import numpy as np
import ml_dtypes


def mxq(x, axis, fmt="e4m3"):
    dtype, down = {"e4m3": (ml_dtypes.float8_e4m3fn, 7), "e5m2": (ml_dtypes.float8_e5m2, 14)}[fmt]
    v = np.moveaxis(np.asarray(x, np.float32).astype(ml_dtypes.bfloat16).astype(np.float64), axis, -1)
    blocks = v.reshape(v.shape[:-1] + (-1, 32))
    amax = np.abs(blocks).max(-1, keepdims=True)
    byte = np.maximum(np.where(amax > 0, np.frexp(amax)[1] - 1 + 127, 0) - down, 1)
    scale = np.exp2(byte - 127.0)
    codes = (blocks / scale).astype(np.float32).astype(dtype).astype(np.float64)
    return np.moveaxis((codes * scale).reshape(v.shape), -1, axis)


WIDE = False


def mx_kscale(k):
    if not WIDE:
        return np.ones(k)
    levels = np.array([18, -18])
    if k % 512:
        return np.exp2(np.random.permutation(np.resize(levels, k // 32))).repeat(32)
    a = np.empty((k // 512, 16))
    for p in range(k // 512):
        a[p, :8] = np.random.permutation(np.resize(levels, 8))
        for g in range(8):
            far = levels[np.abs(levels - a[p, g]) >= 10]
            a[p, g + 8] = far[np.random.randint(len(far))]
    return np.exp2(a.ravel()).repeat(32)


BF16 = ml_dtypes.bfloat16


def bf(x):
    return np.asarray(x, np.float32).astype(BF16)


def f64(x):
    return np.asarray(x).astype(np.float64)


B, D, C = 1024, 48, 1024
EPS_SQRT = 1e-10
EPS_NORM = 1e-12


def outer_rows(f):
    return (f[:, :, None] * f[:, None, :]).reshape(f.shape[0], -1)


def row_norm(f):
    return np.maximum(np.sqrt(np.sum(np.abs(outer_rows(f)) + EPS_SQRT, axis=1)), EPS_NORM)


def setup_inputs():
    s = mx_kscale(B)
    t = (s / np.min(s))[:, None]
    c = np.min(s)
    u = mx_kscale(C)
    n = np.random.standard_normal((B, D))
    feat0 = bf(n + 0.25 * np.sign(n))
    W0 = bf(np.random.standard_normal((C, D * D)))
    b = bf(np.random.standard_normal(C) * 0.3)
    g = bf(np.random.standard_normal((B, C)) * np.exp2(np.random.randint(-6, 1, (B, 1))) * c / t * u)
    norm = row_norm(f64(feat0))
    return {"feat": bf(f64(feat0) * t), "W": bf(f64(W0) / u[:, None]), "b": b,
            "norm": np.asarray(norm, np.float32), "grad_out": g}


def reference(feat, W, b, norm, grad_out):
    f = f64(feat)
    g = f64(grad_out)
    n = f64(norm)[:, None]
    p = outer_rows(f)
    root = np.sqrt(np.abs(p) + EPS_SQRT)
    x = np.sign(p) * root / n
    dx = mxq(g, 1, "e5m2") @ mxq(f64(W), 0, "e4m3")
    dW = mxq(g, 0, "e5m2").T @ mxq(x, 0, "e4m3")
    dy = (dx - x * np.sum(dx * x, axis=1, keepdims=True)) / n
    dp = (0.5 * dy / root).reshape(f.shape[0], f.shape[1], f.shape[1])
    dfeat = np.sum((dp + dp.transpose(0, 2, 1)) * f[:, None, :], axis=2)
    return dfeat, dW

@@ -1,0 +1,473 @@
+from contextlib import ExitStack
+
+import concourse.mybir as mybir
+from concourse.masks import make_identity
+
+B, D, C = 1024, 48, 1024
+DD = D * D
+FLOPS = 2 * 2 * B * C * DD
+BYTES = 2 * B * D + 2 * C * DD + 4 * B + 2 * B * C + 4 * B * D + 4 * C * DD
+EPS = 1e-10
+TINY = 2.0 ** -32
+
+F32 = mybir.dt.float32
+BF16 = mybir.dt.bfloat16
+U32 = mybir.dt.uint32
+U8 = mybir.dt.uint8
+E4 = mybir.dt.float8_e4m3fn_x4
+E5 = mybir.dt.float8_e5m2_x4
+ALU = mybir.AluOpType
+ACT = mybir.ActivationFunctionType
+AX = mybir.AxisListType
+
+P = 128
+H = 6
+NB = D // H
+RP = H // 2
+CHUNKS = [[0], [1, 6], [2, 5], [3, 4]]
+KC = 126
+KOFF = 4 * KC
+KD = NB * RP * H
+KALL = KOFF + KD
+XW = NB * (H * D + H)
+ROWS = D // 2 + RP
+TW = ROWS * 96 + 32
+
+
+def width(b):
+    return D - H * (b + 1)
+
+
+def band_start(b):
+    for c, bands in enumerate(CHUNKS):
+        k = KC * c
+        for o in bands:
+            if o == b:
+                return k
+            k = k + RP * width(o)
+    raise ValueError
+
+
+def tile_bcnnresnet_v_kernel(tc, feat, W, b, norm, grad_out, out_0, out_1):
+    nc = tc.nc
+    V, S, G, PE = nc.vector, nc.scalar, nc.gpsimd, nc.tensor
+    Q1 = G
+    with ExitStack() as ctx:
+        sb = ctx.enter_context(tc.tile_pool(name="sb", bufs=1))
+        ps = ctx.enter_context(tc.psum_pool(name="ps", bufs=1))
+        ctx.enter_context(tc.manual_schedule())
+
+        def zbank(dtype, name):
+            return ps.tile([P, 512 if dtype == F32 else 1024], dtype, name=name, tag="z", bufs=4)
+
+        f = sb.tile([P, 2, 4, D], BF16, name="f", tag="f")
+        nc.sync.dma_start(out=f[:], in_=feat.rearrange("(g p t) d -> p g t d", g=2, t=4))
+        nrm = sb.tile([P, 2, 4], F32, name="nrm")
+        nc.sync.dma_start(out=nrm[:], in_=norm.rearrange("(g p t) -> p g t", g=2, t=4))
+        graw = []
+        for g in range(2):
+            t_ = sb.tile([P, 4, C], BF16, name="graw%d" % g, tag="g%d" % g)
+            nc.sync.dma_start(out=t_[:], in_=grad_out[512 * g:512 * (g + 1), :].rearrange("(p t) c -> p t c", t=4))
+            graw.append(t_)
+        wraw = []
+        for kp in range(2):
+            t_ = sb.tile([P, 4, DD], BF16, name="wraw%d" % kp, tag="w%d" % kp, align_bytes=64)
+            nc.sync.dma_start(out=t_[:], in_=W[512 * kp:512 * (kp + 1), :].rearrange("(p t) c -> p t c", t=4))
+            wraw.append(t_)
+
+        idb = sb.tile([P, P], BF16, name="idb")
+        make_identity(nc, idb[:])
+        idf = sb.tile([P, P], F32, name="idf")
+        make_identity(nc, idf[:])
+
+        fl = f[:].rearrange("p g t d -> p (g t d)")
+        NS = 8 * D
+        absf = sb.tile([P, NS], BF16, name="absf")
+        S.activation(out=absf[:], in_=fl, func=ACT.Abs)
+        sgn = sb.tile([P, NS], BF16, name="sgn")
+        S.activation(out=sgn[:], in_=fl, func=ACT.Sign)
+        aj = sb.tile([P, 2, D, 4, 2], BF16, name="aj")
+        S.copy(out=aj[:], in_=absf[:].rearrange("p (g t j) -> p g j t", g=2, t=4).unsqueeze(4).to_broadcast([P, 2, D, 4, 2]))
+        zd = sb.tile([P, NS], BF16, name="zd", tag="zd")
+        V.tensor_scalar(out=zd[:], in0=fl, scalar1=0.0, scalar2=TINY, op0=ALU.is_equal, op1=ALU.mult)
+        rn = sb.tile([P, 8], F32, name="rn")
+        V.reciprocal(out=rn[:], in_=nrm[:].rearrange("p g t -> p (g t)"))
+        amax = sb.tile([P, 2], F32, name="amax")
+        V.tensor_reduce(out=amax[:], in_=absf[:].rearrange("p (g m) -> p g m", g=2), axis=AX.X, op=ALU.max)
+        sh = sb.tile([P, NS], BF16, name="sh", tag="sh")
+        V.tensor_tensor(out=sh[:], in0=sgn[:], in1=zd[:], op=ALU.add)
+        V.tensor_scalar(out=amax[:], in0=amax[:], scalar1=1e-5, scalar2=0.25, op0=ALU.max, op1=ALU.mult)
+        nu = sb.tile([P, 2], F32, name="nu")
+        V.reciprocal(out=nu[:], in_=amax[:])
+        nu2 = sb.tile([P, 2], F32, name="nu2")
+        V.tensor_tensor(out=nu2[:], in0=nu[:], in1=nu[:], op=ALU.mult)
+        rnu = sb.tile([P, 2, 4], F32, name="rnu")
+        V.tensor_tensor(out=rnu[:], in0=rn[:].rearrange("p (g t) -> p g t", g=2), in1=nu[:].unsqueeze(2).to_broadcast([P, 2, 4]), op=ALU.mult)
+        enu = sb.tile([P, 2], F32, name="enu")
+        V.tensor_scalar(out=enu[:], in0=nu2[:], scalar1=EPS, scalar2=None, op0=ALU.mult)
+        cst = ps.tile([P, 1024], BF16, name="cst", tag="cst")
+        ai = cst[:, 0:384].rearrange("p (g r t e) -> p g r t e", g=2, t=4, e=2)
+        si = cst[:, 384:768].rearrange("p (g r t e) -> p g r t e", g=2, t=4, e=2)
+        for src, dst in ((absf, ai), (sh, si)):
+            for g in range(2):
+                PE.matmul(out=dst[:, g], lhsT=idb[:],
+                          rhs=src[:].rearrange("p (g t r e) -> p g r t e", g=2, t=4, e=2)[:, g], start=True, stop=True)
+        sjn = sb.tile([P, 2, D, 4, 2], F32, name="sjn")
+        for g in range(2):
+            G.tensor_tensor(out=sjn[:, g],
+                            in0=sh[:].rearrange("p (g t j) -> p g j t", g=2, t=4)[:, g].unsqueeze(3).to_broadcast([P, D, 4, 2]),
+                            in1=rnu[:, g].unsqueeze(1).unsqueeze(3).to_broadcast([P, D, 4, 2]), op=ALU.mult)
+
+        sis = sb.tile([P, D // 2, 4, 2], BF16, name="sis")
+        S.copy(out=sis[:], in_=sh[:].rearrange("p (g t r e) -> p g r t e", g=2, t=4, e=2)[:, 1])
+        qq = [sb.tile([P, KALL, 4, 2], F32, name="q%d" % g) for g in range(2)]
+        grp = [sb.tile([P, 2048], BF16, name="grp%d" % i, align_bytes=64) for i in range(4)]
+        wc = [sb.tile([P, 5 * 512], U32, name="wc%d" % i, align_bytes=64) for i in range(2)]
+        ws = [sb.tile([P, 5 * 512], U8, name="ws%d" % i, align_bytes=64) for i in range(2)]
+        gtc = sb.tile([P, 2048], U32, name="gtc", align_bytes=64)
+        gts = sb.tile([P, 2048], U8, name="gts", align_bytes=64)
+        gsc = sb.tile([P, 2048], U32, name="gsc", align_bytes=64)
+        gss = sb.tile([P, 2048], U8, name="gss", align_bytes=64)
+        xc = [sb.tile([P, DD], U32, name="xc%d" % i, align_bytes=64) for i in range(2)]
+        xs = [sb.tile([P, DD], U8, name="xs%d" % i, align_bytes=64) for i in range(2)]
+        esum = sb.tile([P, 8, 3], F32, name="esum")
+        for i in (2, 3):
+            G.memset(grp[i][:].rearrange("p (e k) -> p e k", e=2)[:, :, 4 * 2 * KC:1024], 0.0)
+        state = {"grp": 0}
+        tiles = {}
+
+        def next_grp():
+            state["grp"] = state["grp"] + 1
+            return grp[(state["grp"] - 1) % 4]
+
+        def quant(src, codes, scales, fmt):
+            V.quantize_mx(out=codes.bitcast(fmt), scales=scales, in_=src)
+
+        def gt_fill(pair):
+            buf = next_grp()
+            for h in range(2):
+                tau = 2 * pair + h
+                words = graw[tau // 4][:, tau % 4, :].bitcast(F32)
+                bank = zbank(F32, "gtb")
+                for kp in range(2):
+                    for u in range(2):
+                        PE.transpose(bank[:, 128 * (2 * kp + u):128 * (2 * kp + u + 1)],
+                                     words[:, 256 * kp + u:256 * (kp + 1):2], idf[:])
+                S.copy(out=buf[:, 1024 * h:1024 * (h + 1)].bitcast(F32).rearrange("p (k n u) -> p k n u", k=2, u=2),
+                       in_=bank[:].rearrange("p (k u n) -> p k n u", k=2, u=2))
+            return lambda: quant(buf[:], gtc[:, 512 * pair:512 * (pair + 1)], gts[:, 512 * pair:512 * (pair + 1)], E5)
+
+        def gs_fill(piece):
+            g, half = divmod(piece, 2)
+            buf = next_grp()
+            for h in range(2):
+                bank = zbank(BF16, "gsb")
+                for m in range(2):
+                    c0 = 512 * half + 256 * h + 128 * m
+                    PE.matmul(out=bank[:, 512 * m:512 * (m + 1)].rearrange("p (c t) -> p c t", t=4), lhsT=idb[:],
+                              rhs=graw[g][:, :, c0:c0 + 128].rearrange("p t c -> p c t"), start=True, stop=True)
+                S.copy(out=buf[:, 1024 * h:1024 * (h + 1)], in_=bank[:])
+            return lambda: quant(buf[:], gsc[:, 512 * piece:512 * (piece + 1)], gss[:, 512 * piece:512 * (piece + 1)], E5)
+
+        def w_fill(kp, piece):
+            buf = next_grp()
+            w4 = wraw[kp][:].rearrange("p t (r e j) -> p r e j t", e=2, j=D)
+            wt = wraw[kp][:].rearrange("p t (j i) -> p j i t", i=D)
+            halves = buf[:].rearrange("p (e k t) -> p e k t", e=2, t=4)
+            for h in range(2):
+                bank = zbank(BF16, "wb")
+                if piece < 2:
+                    view = bank[:].rearrange("p (e k t) -> p e k t", e=2, t=4)
+                    for bd in CHUNKS[2 * piece + h]:
+                        k0, w = band_start(bd) % KC, width(bd)
+                        for e in range(2):
+                            PE.matmul(out=view[:, e, k0:k0 + RP * w, :].rearrange("p (r j) t -> p r j t", r=RP), lhsT=idb[:],
+                                      rhs=w4[:, RP * bd:RP * bd + RP, e, D - w:D, :], start=True, stop=True)
+                    S.copy(out=halves[:, :, KC * h:KC * (h + 1), :], in_=view[:, :, 0:KC, :])
+                elif piece < 4:
+                    view = bank[:].rearrange("p (k e t) -> p k e t", e=2, t=4)
+                    for bd in CHUNKS[2 * (piece - 2) + h]:
+                        k0, w = band_start(bd) % KC, width(bd)
+                        for r in range(RP):
+                            i0 = H * bd + 2 * r
+                            PE.matmul(out=view[:, k0 + r * w:k0 + (r + 1) * w], lhsT=idb[:],
+                                      rhs=wt[:, D - w:D, i0:i0 + 2, :], start=True, stop=True)
+                    S.copy(out=halves[:, :, KC * h:KC * (h + 1), :], in_=view[:, 0:KC].rearrange("p k e t -> p e k t"))
+                else:
+                    view = bank[:, 0:4 * KD].rearrange("p (b r j t) -> p b r j t", b=NB, r=RP, t=4)
+                    for bd in range(NB):
+                        PE.matmul(out=view[:, bd], lhsT=idb[:],
+                                  rhs=w4[:, RP * bd:RP * bd + RP, h, H * bd:H * bd + H, :], start=True, stop=True)
+                    S.copy(out=buf[:, 1024 * h:1024 * h + 4 * KD], in_=bank[:, 0:4 * KD])
+            cols = slice(512 * piece, 512 * (piece + 1))
+            return lambda: quant(buf[:], wc[kp][:, cols], ws[kp][:, cols], E4)
+
+        def parts(ap, c, base):
+            if c == 4:
+                return [(None, ap[:, KOFF - base:KOFF - base + KD].rearrange("p (b r j) t e -> p b r j t e", b=NB, r=RP))]
+            return [(bd, ap[:, band_start(bd) - base:band_start(bd) - base + RP * width(bd)]
+                     .rearrange("p (r j) t e -> p r j t e", r=RP)) for bd in CHUNKS[c]]
+
+        def by_row(vec, bd):
+            if bd is None:
+                return vec.rearrange("p (b r) t e -> p b r t e", r=RP).unsqueeze(3).to_broadcast([P, NB, RP, H, 4, 2])
+            return vec[:, RP * bd:RP * bd + RP].unsqueeze(2).to_broadcast([P, RP, width(bd), 4, 2])
+
+        def by_col(vec, bd):
+            if bd is None:
+                return vec.rearrange("p (b j) t e -> p b j t e", j=H).unsqueeze(2).to_broadcast([P, NB, RP, H, 4, 2])
+            return vec[:, D - width(bd):D].unsqueeze(1).to_broadcast([P, RP, width(bd), 4, 2])
+
+        def fwd_a(g, c):
+            n = KD if c == 4 else KC
+            a = sb.tile([P, KD, 4, 2], F32, name="a", tag="a", bufs=3)
+            tiles["a", g, c] = a
+            for bd, part in parts(a, c, KC * c):
+                V.tensor_tensor(out=part, in0=by_row(ai[:, g], bd), in1=by_col(aj[:, g], bd), op=ALU.mult)
+            S.activation(out=qq[g][:, KC * c:KC * c + n], in_=a[:, 0:n], func=ACT.Abs_reciprocal_sqrt, bias=enu[:, g:g + 1], scale=nu2[:, g:g + 1])
+            for bd, part in parts(qq[g], c, 0):
+                Q1.tensor_tensor(out=part, in0=part, in1=by_col(sjn[:, g], bd), op=ALU.mult)
+
+        def fwd_q(g, c):
+            for bd, part in parts(qq[g], c, 0):
+                if (g, c) in Q2G:
+                    G.tensor_tensor(out=part, in0=part, in1=by_row(sis[:], bd), op=ALU.mult)
+                else:
+                    V.tensor_tensor(out=part, in0=by_row(si[:, g], bd), in1=part, op=ALU.mult)
+
+        def fwd_x(g, c):
+            if ("x", g) not in tiles:
+                tiles["x", g] = sb.tile([P, XW, 4], BF16, name="x%d" % g, tag="x0" if g == 0 else "w0", align_bytes=64)
+            x = tiles["x", g]
+            a = tiles["a", g, c]
+            if c == 4:
+                xd = sb.tile([P, 2, KD, 4], BF16, name="xd", tag="xd")
+                for e in range(2):
+                    V.scalar_tensor_tensor(out=xd[:, e], in0=a[:, :, :, e], scalar=EPS, in1=qq[g][:, KOFF:KALL, :, e],
+                                           op0=ALU.add, op1=ALU.mult)
+                skew = x[:].rearrange("p (b y) t -> p b y t", b=NB)[:, :, 0:H * D, :].rearrange("p b (r e j) t -> p e b r j t", r=RP, e=2)
+                for e in range(2):
+                    S.copy(out=skew[:, e, :, :, 0:H, :], in_=xd[:, e].rearrange("p (b r j) t -> p b r j t", b=NB, r=RP))
+                return
+            x4 = x[:, 0:DD, :].rearrange("p (r e j) t -> p r e j t", e=2, j=D)
+            for (bd, pa), (bd2, pq) in zip(parts(a, c, KC * c), parts(qq[g], c, 0)):
+                for e in range(2):
+                    V.scalar_tensor_tensor(out=x4[:, RP * bd:RP * bd + RP, e, D - width(bd):D, :], in0=pa[:, :, :, :, e], scalar=EPS,
+                                           in1=pq[:, :, :, :, e], op0=ALU.add, op1=ALU.mult)
+
+        def mirror(g, bands):
+            xn = tiles["x", g][:, 0:DD, :].rearrange("p (i j) t -> p i j t", j=D)
+            for bd in bands:
+                w = width(bd)
+                S.copy(out=xn[:, D - w:D, H * bd:H * bd + H, :], in_=xn[:, H * bd:H * bd + H, D - w:D, :].rearrange("p i j t -> p j i t"))
+
+        def x_quant(g, q):
+            n = 512 if q < 4 else 256
+            quant(tiles["x", g][:, 512 * q:512 * q + n, :].rearrange("p c t -> p (c t)"),
+                  xc[g][:, 512 * q:512 * q + n], xs[g][:, 512 * q:512 * q + n], E4)
+
+        def dx(tau, bks=(0, 1, 2)):
+            banks = tiles.setdefault(("z", tau), [])
+            for bk in bks:
+                bank = zbank(F32, "zb")
+                passes = [(kp, pc) for pc in ((bk, bk + 2) if bk < 2 else (4,)) for kp in range(2)]
+                for n, (kp, pc) in enumerate(passes):
+                    st = slice(256 * tau + 128 * kp, 256 * tau + 128 * (kp + 1))
+                    mv = slice(512 * pc, 512 * (pc + 1))
+                    PE.matmul_mx(out=bank[:], lhsT=gtc[:, st].bitcast(E5), lhsT_scale=gts[:, st], rhs=wc[kp][:, mv].bitcast(E4),
+                                 rhs_scale=ws[kp][:, mv], start=(n == 0), stop=(n == len(passes) - 1))
+                banks.append(bank)
+
+        def m_pass(tau):
+            g, t = divmod(tau, 4)
+            m = sb.tile([P, KALL, 2], F32, name="m", tag="m", bufs=2)
+            tiles["m", tau] = m
+            for bk, bank in enumerate(tiles["z", tau]):
+                k0, n = 2 * KC * bk, (2 * KC if bk < 2 else KD)
+                V.scalar_tensor_tensor(out=m[:, k0:k0 + n, :], in0=bank[:].rearrange("p (e k) -> p k e", e=2)[:, 0:n, :], scalar=1.0,
+                                       in1=qq[g][:, k0:k0 + n, t, :], op0=ALU.mult, op1=ALU.mult, accum_out=esum[:, tau, bk:bk + 1])
+
+        def u_pass(tau):
+            m = tiles["m", tau]
+            tt = tiles["t"][:, tau % 2, :]
+            a2 = tiles["a2"][:, tau]
+            rows = tt[:, 0:ROWS * 96].rearrange("p (k R e s) -> p k R e s", R=D // 2, e=2, s=2)
+            for bd in [o for c in CHUNKS for o in c]:
+                w, k0, r0 = width(bd), band_start(bd), RP * bd
+                mb = m[:, k0:k0 + RP * w, :].rearrange("p (r jp jj) e -> p r jp jj e", r=RP, jj=2)
+                V.tensor_tensor(out=rows[:, r0:r0 + RP, r0 + RP:D // 2], in0=mb.rearrange("p r jp jj e -> p r jp e jj"),
+                                in1=a2[:, 2 * r0:2 * r0 + H, :].rearrange("p (r e) s -> p r e s", e=2).unsqueeze(2)
+                                .to_broadcast([P, RP, w // 2, 2, 2]), op=ALU.mult)
+                V.tensor_tensor(out=rows[:, r0 + RP:D // 2, r0:r0 + RP].rearrange("p jp r jj e -> p r jp jj e"), in0=mb,
+                                in1=a2[:, D - w:D, :].rearrange("p (jp jj) s -> p jp jj s", jj=2).unsqueeze(1)
+                                .to_broadcast([P, RP, w // 2, 2, 2]), op=ALU.mult)
+            md = m[:, KOFF:KALL, :].rearrange("p (b r jp jj) e -> p b r jp jj e", b=NB, r=RP, jj=2)
+            skew = tt[:, 0:NB * 300].rearrange("p (b y) -> p b y", b=NB)[:, :, 0:288].rearrange("p b (r y) -> p b r y", r=RP)[:, :, :, 0:12]
+            V.tensor_tensor(out=skew.rearrange("p b r (jp e jj) -> p b r jp e jj", e=2, jj=2), in0=md.rearrange("p b r jp jj e -> p b r jp e jj"),
+                            in1=a2.rearrange("p (b r e) s -> p b r e s", r=RP, e=2).unsqueeze(3).to_broadcast([P, NB, RP, RP, 2, 2]),
+                            op=ALU.mult)
+            V.tensor_tensor(out=rows[:, D // 2:ROWS].rearrange("p jp (b r) jj e -> p b r jp jj e", r=RP), in0=md,
+                            in1=a2.rearrange("p (b jp jj) s -> p b jp jj s", jp=RP, jj=2).unsqueeze(2).to_broadcast([P, NB, RP, RP, 2, 2]),
+                            op=ALU.mult)
+
+        def fold(tau, eng, n_from):
+            tt = tiles["t"][:, tau % 2, :]
+            n_to = (n_from + 1) // 2
+            k = n_from - n_to
+            eng.tensor_tensor(out=tt[:, 0:96 * k], in0=tt[:, 0:96 * k], in1=tt[:, 96 * n_to:96 * n_from], op=ALU.add)
+            return n_to
+
+        def t_sum(tau, lo, hi, last):
+            g, t = divmod(tau, 4)
+            if ("acc", g) not in tiles:
+                tiles["acc", g] = ps.tile([P, 512], F32, name="acc", tag="acc")
+            tt = tiles["t"][:, tau % 2, :]
+            for k in range(lo, hi):
+                PE.matmul(out=tiles["acc", g][:, 128 * t:128 * (t + 1)], lhsT=tt[:, 96 * k:96 * k + 128], rhs=idf[:],
+                          start=(k == 0), stop=(k == last - 1), is_transpose=True)
+
+        def back(g):
+            accs = sb.tile([P, 512], F32, name="accs", tag="xd")
+            S.copy(out=accs[:], in_=tiles["acc", g][:])
+            bank = zbank(F32, "bb")
+            for t in range(4):
+                PE.transpose(bank[:, 96 * t:96 * t + 128], accs[:, 128 * t:128 * (t + 1)], idf[:])
+            tiles["bb", g] = bank
+
+        def finish(g):
+            bank = tiles["bb", g]
+            sl = slice(4 * D * g, 4 * D * (g + 1))
+            bs = sb.tile([P, 4 * D], F32, name="bs", tag="neg")
+            V.tensor_reduce(out=bs[:].rearrange("p (r e) -> p r e", e=2),
+                            in_=bank[:, 0:384].rearrange("p (r s e) -> p r e s", s=2, e=2), axis=AX.X, op=ALU.add)
+            es = sb.tile([P, 4], F32, name="es", tag="es")
+            V.tensor_reduce(out=es[:], in_=esum[:, 4 * g:4 * g + 4, :], axis=AX.X, op=ALU.add)
+            ab = sb.tile([P, 4, D], F32, name="ab", tag="zd")
+            V.tensor_tensor(out=ab[:].rearrange("p t m -> p (t m)"), in0=bs[:], in1=absf[:, sl], op=ALU.mult)
+            t1 = sb.tile([P, 4 * D], F32, name="t1", tag="f")
+            V.tensor_tensor(out=t1[:], in0=bs[:], in1=tiles["hs"][:, sl], op=ALU.mult)
+            s1 = sb.tile([P, 4], F32, name="s1", tag="s1")
+            V.tensor_reduce(out=s1[:], in_=ab[:], axis=AX.X, op=ALU.add)
+            s2 = sb.tile([P, 4], F32, name="s2", tag="s2")
+            V.scalar_tensor_tensor(out=s2[:], in0=es[:], scalar=2 * EPS, in1=s1[:], op0=ALU.mult, op1=ALU.add)
+            V.tensor_tensor(out=ab[:], in0=tiles["ks"][:, sl].rearrange("p (t m) -> p t m", t=4),
+                            in1=s2[:].unsqueeze(2).to_broadcast([P, 4, D]), op=ALU.mult)
+            res = sb.tile([P, 4, D], F32, name="res", tag="sh")
+            V.tensor_tensor(out=res[:].rearrange("p t m -> p (t m)"), in0=t1[:], in1=ab[:].rearrange("p t m -> p (t m)"), op=ALU.subtract)
+            nc.sync.dma_start(out=out_0[512 * g:512 * (g + 1), :].rearrange("(p t) d -> p t d", t=4), in_=res[:])
+
+        def late_consts():
+            a2s = sb.tile([P, NS, 2], BF16, name="a2s", tag="xd")
+            S.copy(out=a2s[:], in_=absf[:].unsqueeze(2).to_broadcast([P, NS, 2]))
+            asum = sb.tile([P, 8], F32, name="asum")
+            V.tensor_reduce(out=asum[:], in_=absf[:].rearrange("p (n m) -> p n m", m=D), axis=AX.X, op=ALU.add)
+            hr = sb.tile([P, NS], BF16, name="hr")
+            h0 = sb.tile([P, NS], BF16, name="h0", tag="neg")
+            V.tensor_scalar(out=h0[:], in0=fl, scalar1=0.0, scalar2=0.5 / TINY, op0=ALU.is_equal, op1=ALU.mult)
+            k1 = sb.tile([P, 8], F32, name="k1")
+            V.scalar_tensor_tensor(out=k1[:], in0=asum[:], scalar=0.5, in1=rn[:], op0=ALU.mult, op1=ALU.mult)
+            V.scalar_tensor_tensor(out=hr[:], in0=sgn[:], scalar=0.5, in1=h0[:], op0=ALU.mult, op1=ALU.add)
+            k2 = sb.tile([P, 8], F32, name="k2")
+            V.tensor_tensor(out=k2[:], in0=k1[:], in1=rn[:], op=ALU.mult)
+            c2 = ps.tile([P, 1024], BF16, name="c2", tag="c2")
+            for h in range(2):
+                PE.matmul(out=c2[:, 384 * h:384 * (h + 1)], lhsT=idb[:],
+                          rhs=a2s[:].rearrange("p m s -> p (m s)")[:, 384 * h:384 * (h + 1)], start=True, stop=True)
+            ks = sb.tile([P, 8, D], F32, name="ks")
+            G.tensor_tensor(out=ks[:], in0=sgn[:].rearrange("p (n m) -> p n m", m=D),
+                            in1=k2[:].unsqueeze(2).to_broadcast([P, 8, D]), op=ALU.mult)
+            tiles["a2"] = c2[:, 0:768].rearrange("p (n m s) -> p n m s", n=8, s=2)
+            tiles["hs"] = hr
+            tiles["ks"] = ks[:].rearrange("p n m -> p (n m)")
+
+        def make_t():
+            tiles["t"] = sb.tile([P, 2, TW], F32, name="t", tag="w1", align_bytes=64)
+            G.memset(tiles["t"][:, :, ROWS * 96:TW], 0.0)
+
+        def dw(unit):
+            ct, q = divmod(unit, 5)
+            if ct < 2 and q == 0:
+                tiles["st", ct] = sb.tile([P, DD], F32, name="st%d" % ct, tag="g%d" % ct)[:]
+            if ct == 2 and q == 0:
+                both = sb.tile([P, 2, DD], F32, name="st2", tag="x0", align_bytes=64)
+                tiles["st", 2], tiles["st", 3] = both[:, 0, :], both[:, 1, :]
+            st = tiles["st", ct % 4]
+            c0 = min(512 * q, DD - 512)
+            bank = ps.tile([P, 512], F32, name="dwb", tag="dw" if unit % 2 == 0 else "cst")
+            for g in range(2):
+                sl = slice(1024 * g + 128 * ct, 1024 * g + 128 * (ct + 1))
+                PE.matmul_mx(out=bank[:], lhsT=gsc[:, sl].bitcast(E5), lhsT_scale=gss[:, sl], rhs=xc[g][:, c0:c0 + 512].bitcast(E4),
+                             rhs_scale=xs[g][:, c0:c0 + 512], start=(g == 0), stop=(g == 1))
+            S.copy(out=st[:, 512 * q:c0 + 512], in_=bank[:, 512 * q - c0:512])
+            if q in (1, 4):
+                lo = 0 if q == 1 else 1024
+                nc.sync.dma_start(out=out_1[128 * ct:128 * (ct + 1), lo:c0 + 512], in_=st[:, lo:c0 + 512])
+
+        Q2G = {(1, c) for c in range(1, 5)}
+        chunks = [(g, c) for g in range(2) for c in range(5)]
+        fills = {0: [lambda: gt_fill(0), lambda: gt_fill(1)],
+                 6: [lambda: gs_fill(0), lambda: gs_fill(1)], 7: [lambda: gs_fill(2), lambda: gs_fill(3)],
+                 8: [lambda: gt_fill(2), lambda: gt_fill(3)]}
+        for n in range(5):
+            fills[1 + n] = [lambda m=m: w_fill(m // 5, m % 5) for m in (2 * n, 2 * n + 1)]
+        pending = []
+        fwd_a(0, 0)
+        for s in range(11):
+            if s + 1 < 10:
+                fwd_a(*chunks[s + 1])
+            if s >= 1:
+                fwd_x(*chunks[s - 1])
+            for q in pending:
+                q()
+            if s == 1:
+                late_consts()
+            if s == 6:
+                make_t()
+                dx(0)
+            if s == 7:
+                for q in range(5):
+                    x_quant(0, q)
+            pending = [fl_() for fl_ in fills.get(s, [])]
+            if s == 5:
+                mirror(0, range(0, 2))
+            if s == 6:
+                mirror(0, range(2, 7))
+            if s == 9:
+                mirror(1, range(0, 7))
+            if s < 10:
+                fwd_q(*chunks[s])
+            if s in (6, 7, 8, 9):
+                m_pass(s - 6)
+                dx(s - 5)
+                u_pass(s - 6)
+                if s > 6:
+                    t_sum(s - 7, 0, ROWS, ROWS)
+        for q in range(5):
+            x_quant(1, q)
+        rows = {3: ROWS}
+        unit = 0
+        for tau in range(4, 8):
+            m_pass(tau)
+            n = rows[tau - 1]
+            for step in range(3):
+                dw(unit)
+                dw(unit + 1)
+                if tau < 7:
+                    dx(tau + 1, (step,))
+                dw(unit + 2)
+                unit = unit + 3
+                if step != 1:
+                    t_sum(tau - 1, 0 if step == 0 else n // 2, n // 2 if step == 0 else n, n)
+            if tau == 4:
+                back(0)
+            u_pass(tau)
+            rows[tau] = fold(tau, V, fold(tau, V, ROWS))
+            if tau == 5:
+                finish(0)
+        dw(36)
+        dw(37)
+        t_sum(7, 0, rows[7], rows[7])
+        back(1)
+        dw(38)
+        dw(39)
+        finish(1)

@@ -25,6 +25,7 @@ H = 6
 NB = D // H
 RP = H // 2
 CHUNKS = [[0], [1, 6], [2, 5], [3, 4]]
+STEPS = [[0], [1, (0, 2)], [2, (2, 4)], [3, 4], [5, 6, (4, 8)]]
 KC = 126
 KOFF = 4 * KC
 KD = NB * RP * H
@@ -55,7 +56,6 @@ def tile_bcnnresnet_v_kernel(tc, feat, W, b, norm, grad_out, out_0, out_1):
     with ExitStack() as ctx:
         sb = ctx.enter_context(tc.tile_pool(name="sb", bufs=1))
         ps = ctx.enter_context(tc.psum_pool(name="ps", bufs=1))
-        ctx.enter_context(tc.manual_schedule())
 
         def zbank(dtype, name):
             return ps.tile([P, 512 if dtype == F32 else 1024], dtype, name=name, tag="z", bufs=4)
@@ -64,16 +64,10 @@ def tile_bcnnresnet_v_kernel(tc, feat, W, b, norm, grad_out, out_0, out_1):
         nc.sync.dma_start(out=f[:], in_=feat.rearrange("(g p t) d -> p g t d", g=2, t=4))
         nrm = sb.tile([P, 2, 4], F32, name="nrm")
         nc.sync.dma_start(out=nrm[:], in_=norm.rearrange("(g p t) -> p g t", g=2, t=4))
-        graw = []
-        for g in range(2):
-            t_ = sb.tile([P, 4, C], BF16, name="graw%d" % g, tag="g%d" % g)
-            nc.sync.dma_start(out=t_[:], in_=grad_out[512 * g:512 * (g + 1), :].rearrange("(p t) c -> p t c", t=4))
-            graw.append(t_)
-        wraw = []
-        for kp in range(2):
-            t_ = sb.tile([P, 4, DD], BF16, name="wraw%d" % kp, tag="w%d" % kp, align_bytes=64)
-            nc.sync.dma_start(out=t_[:], in_=W[512 * kp:512 * (kp + 1), :].rearrange("(p t) c -> p t c", t=4))
-            wraw.append(t_)
+        graw = [sb.tile([P, 4, C], BF16, name="graw%d" % g, tag="g%d" % g) for g in range(2)]
+        wraw = [sb.tile([P, 4, DD], BF16, name="wraw%d" % kp, tag="w%d" % kp, align_bytes=64) for kp in range(2)]
+        for dst, src, h in ((graw, grad_out, 0), (wraw, W, 0), (wraw, W, 1), (graw, grad_out, 1)):
+            nc.sync.dma_start(out=dst[h][:], in_=src[512 * h:512 * (h + 1), :].rearrange("(p t) c -> p t c", t=4))
 
         idb = sb.tile([P, P], BF16, name="idb")
         make_identity(nc, idb[:])
@@ -113,10 +107,12 @@ def tile_bcnnresnet_v_kernel(tc, feat, W, b, norm, grad_out, out_0, out_1):
                 PE.matmul(out=dst[:, g], lhsT=idb[:],
                           rhs=src[:].rearrange("p (g t r e) -> p g r t e", g=2, t=4, e=2)[:, g], start=True, stop=True)
         sjn = sb.tile([P, 2, D, 4, 2], F32, name="sjn")
-        for g in range(2):
-            G.tensor_tensor(out=sjn[:, g],
+
+        def make_sjn(g):
+            V.tensor_tensor(out=sjn[:, g],
                             in0=sh[:].rearrange("p (g t j) -> p g j t", g=2, t=4)[:, g].unsqueeze(3).to_broadcast([P, D, 4, 2]),
                             in1=rnu[:, g].unsqueeze(1).unsqueeze(3).to_broadcast([P, D, 4, 2]), op=ALU.mult)
+
 
         sis = sb.tile([P, D // 2, 4, 2], BF16, name="sis")
         S.copy(out=sis[:], in_=sh[:].rearrange("p (g t r e) -> p g r t e", g=2, t=4, e=2)[:, 1])
@@ -166,7 +162,7 @@ def tile_bcnnresnet_v_kernel(tc, feat, W, b, norm, grad_out, out_0, out_1):
                     c0 = 512 * half + 256 * h + 128 * m
                     PE.matmul(out=bank[:, 512 * m:512 * (m + 1)].rearrange("p (c t) -> p c t", t=4), lhsT=idb[:],
                               rhs=graw[g][:, :, c0:c0 + 128].rearrange("p t c -> p c t"), start=True, stop=True)
-                S.copy(out=buf[:, 1024 * h:1024 * (h + 1)], in_=bank[:])
+                S.copy(out=buf[:, 1024 * h:1024 * (h + 1)].bitcast(F32), in_=bank[:].bitcast(F32))
             return lambda: quant(buf[:], gsc[:, 512 * piece:512 * (piece + 1)], gss[:, 512 * piece:512 * (piece + 1)], E5)
 
         def w_fill(kp, piece):
@@ -183,7 +179,7 @@ def tile_bcnnresnet_v_kernel(tc, feat, W, b, norm, grad_out, out_0, out_1):
                         for e in range(2):
                             PE.matmul(out=view[:, e, k0:k0 + RP * w, :].rearrange("p (r j) t -> p r j t", r=RP), lhsT=idb[:],
                                       rhs=w4[:, RP * bd:RP * bd + RP, e, D - w:D, :], start=True, stop=True)
-                    S.copy(out=halves[:, :, KC * h:KC * (h + 1), :], in_=view[:, :, 0:KC, :])
+                    S.copy(out=halves[:, :, KC * h:KC * (h + 1), :].bitcast(F32), in_=view[:, :, 0:KC, :].bitcast(F32))
                 elif piece < 4:
                     view = bank[:].rearrange("p (k e t) -> p k e t", e=2, t=4)
                     for bd in CHUNKS[2 * (piece - 2) + h]:
@@ -192,68 +188,87 @@ def tile_bcnnresnet_v_kernel(tc, feat, W, b, norm, grad_out, out_0, out_1):
                             i0 = H * bd + 2 * r
                             PE.matmul(out=view[:, k0 + r * w:k0 + (r + 1) * w], lhsT=idb[:],
                                       rhs=wt[:, D - w:D, i0:i0 + 2, :], start=True, stop=True)
-                    S.copy(out=halves[:, :, KC * h:KC * (h + 1), :], in_=view[:, 0:KC].rearrange("p k e t -> p e k t"))
+                    S.copy(out=halves[:, :, KC * h:KC * (h + 1), :].bitcast(F32), in_=view[:, 0:KC].bitcast(F32).rearrange("p k e t -> p e k t"))
                 else:
                     view = bank[:, 0:4 * KD].rearrange("p (b r j t) -> p b r j t", b=NB, r=RP, t=4)
                     for bd in range(NB):
                         PE.matmul(out=view[:, bd], lhsT=idb[:],
                                   rhs=w4[:, RP * bd:RP * bd + RP, h, H * bd:H * bd + H, :], start=True, stop=True)
-                    S.copy(out=buf[:, 1024 * h:1024 * h + 4 * KD], in_=bank[:, 0:4 * KD])
+                    S.copy(out=buf[:, 1024 * h:1024 * h + 4 * KD].bitcast(F32), in_=bank[:, 0:4 * KD].bitcast(F32))
             cols = slice(512 * piece, 512 * (piece + 1))
             return lambda: quant(buf[:], wc[kp][:, cols], ws[kp][:, cols], E4)
 
-        def parts(ap, c, base):
-            if c == 4:
-                return [(None, ap[:, KOFF - base:KOFF - base + KD].rearrange("p (b r j) t e -> p b r j t e", b=NB, r=RP))]
-            return [(bd, ap[:, band_start(bd) - base:band_start(bd) - base + RP * width(bd)]
-                     .rearrange("p (r j) t e -> p r j t e", r=RP)) for bd in CHUNKS[c]]
+        def size(part):
+            return RP * width(part) if isinstance(part, int) else RP * H * (part[1] - part[0])
 
-        def by_row(vec, bd):
-            if bd is None:
-                return vec.rearrange("p (b r) t e -> p b r t e", r=RP).unsqueeze(3).to_broadcast([P, NB, RP, H, 4, 2])
-            return vec[:, RP * bd:RP * bd + RP].unsqueeze(2).to_broadcast([P, RP, width(bd), 4, 2])
+        def shaped(ap, part, k0):
+            if isinstance(part, int):
+                return ap[:, k0:k0 + size(part)].rearrange("p (r j) t e -> p r j t e", r=RP)
+            return ap[:, k0:k0 + size(part)].rearrange("p (b r j) t e -> p b r j t e", r=RP, j=H)
 
-        def by_col(vec, bd):
-            if bd is None:
-                return vec.rearrange("p (b j) t e -> p b j t e", j=H).unsqueeze(2).to_broadcast([P, NB, RP, H, 4, 2])
-            return vec[:, D - width(bd):D].unsqueeze(1).to_broadcast([P, RP, width(bd), 4, 2])
+        def q_start(part):
+            return band_start(part) if isinstance(part, int) else KOFF + RP * H * part[0]
+
+        def a_parts(c):
+            starts = [sum(size(o) for o in STEPS[c][:n]) for n in range(len(STEPS[c]))]
+            return list(zip(STEPS[c], starts))
+
+        def by_row(vec, part):
+            if isinstance(part, int):
+                return vec[:, RP * part:RP * part + RP].unsqueeze(2).to_broadcast([P, RP, width(part), 4, 2])
+            return (vec.rearrange("p (b r) t e -> p b r t e", r=RP)[:, part[0]:part[1]].unsqueeze(3)
+                    .to_broadcast([P, part[1] - part[0], RP, H, 4, 2]))
+
+        def by_col(vec, part):
+            if isinstance(part, int):
+                return vec[:, D - width(part):D].unsqueeze(1).to_broadcast([P, RP, width(part), 4, 2])
+            return (vec.rearrange("p (b j) t e -> p b j t e", j=H)[:, part[0]:part[1]].unsqueeze(2)
+                    .to_broadcast([P, part[1] - part[0], RP, H, 4, 2]))
 
         def fwd_a(g, c):
-            n = KD if c == 4 else KC
             a = sb.tile([P, KD, 4, 2], F32, name="a", tag="a", bufs=3)
             tiles["a", g, c] = a
-            for bd, part in parts(a, c, KC * c):
-                V.tensor_tensor(out=part, in0=by_row(ai[:, g], bd), in1=by_col(aj[:, g], bd), op=ALU.mult)
-            S.activation(out=qq[g][:, KC * c:KC * c + n], in_=a[:, 0:n], func=ACT.Abs_reciprocal_sqrt, bias=enu[:, g:g + 1], scale=nu2[:, g:g + 1])
-            for bd, part in parts(qq[g], c, 0):
-                Q1.tensor_tensor(out=part, in0=part, in1=by_col(sjn[:, g], bd), op=ALU.mult)
+            for part, k0 in a_parts(c):
+                V.tensor_tensor(out=shaped(a, part, k0), in0=by_row(ai[:, g], part), in1=by_col(aj[:, g], part), op=ALU.mult)
+
+        def fwd_r(g, c):
+            a = tiles["a", g, c]
+            for part, k0 in a_parts(c):
+                S.activation(out=qq[g][:, q_start(part):q_start(part) + size(part)], in_=a[:, k0:k0 + size(part)],
+                             func=ACT.Abs_reciprocal_sqrt, bias=enu[:, g:g + 1], scale=nu2[:, g:g + 1])
+            for part in STEPS[c]:
+                q = shaped(qq[g], part, q_start(part))
+                G.tensor_tensor(out=q, in0=q, in1=by_col(sjn[:, g], part), op=ALU.mult)
 
         def fwd_q(g, c):
-            for bd, part in parts(qq[g], c, 0):
+            for part in STEPS[c]:
+                q = shaped(qq[g], part, q_start(part))
                 if (g, c) in Q2G:
-                    G.tensor_tensor(out=part, in0=part, in1=by_row(sis[:], bd), op=ALU.mult)
+                    G.tensor_tensor(out=q, in0=q, in1=by_row(sis[:], part), op=ALU.mult)
                 else:
-                    V.tensor_tensor(out=part, in0=by_row(si[:, g], bd), in1=part, op=ALU.mult)
+                    V.tensor_tensor(out=q, in0=by_row(si[:, g], part), in1=q, op=ALU.mult)
 
         def fwd_x(g, c):
             if ("x", g) not in tiles:
                 tiles["x", g] = sb.tile([P, XW, 4], BF16, name="x%d" % g, tag="x0" if g == 0 else "w0", align_bytes=64)
             x = tiles["x", g]
             a = tiles["a", g, c]
-            if c == 4:
-                xd = sb.tile([P, 2, KD, 4], BF16, name="xd", tag="xd")
-                for e in range(2):
-                    V.scalar_tensor_tensor(out=xd[:, e], in0=a[:, :, :, e], scalar=EPS, in1=qq[g][:, KOFF:KALL, :, e],
-                                           op0=ALU.add, op1=ALU.mult)
-                skew = x[:].rearrange("p (b y) t -> p b y t", b=NB)[:, :, 0:H * D, :].rearrange("p b (r e j) t -> p e b r j t", r=RP, e=2)
-                for e in range(2):
-                    S.copy(out=skew[:, e, :, :, 0:H, :], in_=xd[:, e].rearrange("p (b r j) t -> p b r j t", b=NB, r=RP))
-                return
             x4 = x[:, 0:DD, :].rearrange("p (r e j) t -> p r e j t", e=2, j=D)
-            for (bd, pa), (bd2, pq) in zip(parts(a, c, KC * c), parts(qq[g], c, 0)):
-                for e in range(2):
-                    V.scalar_tensor_tensor(out=x4[:, RP * bd:RP * bd + RP, e, D - width(bd):D, :], in0=pa[:, :, :, :, e], scalar=EPS,
-                                           in1=pq[:, :, :, :, e], op0=ALU.add, op1=ALU.mult)
+            skew = x[:].rearrange("p (b y) t -> p b y t", b=NB)[:, :, 0:H * D, :].rearrange("p b (r e j) t -> p e b r j t", r=RP, e=2)
+            for part, k0 in a_parts(c):
+                pa, pq = shaped(a, part, k0), shaped(qq[g], part, q_start(part))
+                if isinstance(part, int):
+                    for e in range(2):
+                        V.scalar_tensor_tensor(out=x4[:, RP * part:RP * part + RP, e, D - width(part):D, :], in0=pa[:, :, :, :, e],
+                                               scalar=EPS, in1=pq[:, :, :, :, e], op0=ALU.add, op1=ALU.mult)
+                    mirror(g, [part])
+                else:
+                    xd = sb.tile([P, 2, part[1] - part[0], RP, H, 4], BF16, name="xd", tag="xd")
+                    for e in range(2):
+                        V.scalar_tensor_tensor(out=xd[:, e], in0=pa[:, :, :, :, :, e], scalar=EPS, in1=pq[:, :, :, :, :, e],
+                                               op0=ALU.add, op1=ALU.mult)
+                    for e in range(2):
+                        S.copy(out=skew[:, e, part[0]:part[1], :, 0:H, :], in_=xd[:, e])
 
         def mirror(g, bands):
             xn = tiles["x", g][:, 0:DD, :].rearrange("p (i j) t -> p i j t", j=D)
@@ -287,26 +302,26 @@ def tile_bcnnresnet_v_kernel(tc, feat, W, b, norm, grad_out, out_0, out_1):
                 V.scalar_tensor_tensor(out=m[:, k0:k0 + n, :], in0=bank[:].rearrange("p (e k) -> p k e", e=2)[:, 0:n, :], scalar=1.0,
                                        in1=qq[g][:, k0:k0 + n, t, :], op0=ALU.mult, op1=ALU.mult, accum_out=esum[:, tau, bk:bk + 1])
 
-        def u_pass(tau):
+        def u_pass(tau, E=V):
             m = tiles["m", tau]
             tt = tiles["t"][:, tau % 2, :]
-            a2 = tiles["a2"][:, tau]
+            a2 = tiles["a2" if E is V else "a2s"][:, tau]
             rows = tt[:, 0:ROWS * 96].rearrange("p (k R e s) -> p k R e s", R=D // 2, e=2, s=2)
             for bd in [o for c in CHUNKS for o in c]:
                 w, k0, r0 = width(bd), band_start(bd), RP * bd
                 mb = m[:, k0:k0 + RP * w, :].rearrange("p (r jp jj) e -> p r jp jj e", r=RP, jj=2)
-                V.tensor_tensor(out=rows[:, r0:r0 + RP, r0 + RP:D // 2], in0=mb.rearrange("p r jp jj e -> p r jp e jj"),
+                E.tensor_tensor(out=rows[:, r0:r0 + RP, r0 + RP:D // 2], in0=mb.rearrange("p r jp jj e -> p r jp e jj"),
                                 in1=a2[:, 2 * r0:2 * r0 + H, :].rearrange("p (r e) s -> p r e s", e=2).unsqueeze(2)
                                 .to_broadcast([P, RP, w // 2, 2, 2]), op=ALU.mult)
-                V.tensor_tensor(out=rows[:, r0 + RP:D // 2, r0:r0 + RP].rearrange("p jp r jj e -> p r jp jj e"), in0=mb,
+                E.tensor_tensor(out=rows[:, r0 + RP:D // 2, r0:r0 + RP].rearrange("p jp r jj e -> p r jp jj e"), in0=mb,
                                 in1=a2[:, D - w:D, :].rearrange("p (jp jj) s -> p jp jj s", jj=2).unsqueeze(1)
                                 .to_broadcast([P, RP, w // 2, 2, 2]), op=ALU.mult)
             md = m[:, KOFF:KALL, :].rearrange("p (b r jp jj) e -> p b r jp jj e", b=NB, r=RP, jj=2)
             skew = tt[:, 0:NB * 300].rearrange("p (b y) -> p b y", b=NB)[:, :, 0:288].rearrange("p b (r y) -> p b r y", r=RP)[:, :, :, 0:12]
-            V.tensor_tensor(out=skew.rearrange("p b r (jp e jj) -> p b r jp e jj", e=2, jj=2), in0=md.rearrange("p b r jp jj e -> p b r jp e jj"),
+            E.tensor_tensor(out=skew.rearrange("p b r (jp e jj) -> p b r jp e jj", e=2, jj=2), in0=md.rearrange("p b r jp jj e -> p b r jp e jj"),
                             in1=a2.rearrange("p (b r e) s -> p b r e s", r=RP, e=2).unsqueeze(3).to_broadcast([P, NB, RP, RP, 2, 2]),
                             op=ALU.mult)
-            V.tensor_tensor(out=rows[:, D // 2:ROWS].rearrange("p jp (b r) jj e -> p b r jp jj e", r=RP), in0=md,
+            E.tensor_tensor(out=rows[:, D // 2:ROWS].rearrange("p jp (b r) jj e -> p b r jp jj e", r=RP), in0=md,
                             in1=a2.rearrange("p (b jp jj) s -> p b jp jj s", jp=RP, jj=2).unsqueeze(2).to_broadcast([P, NB, RP, RP, 2, 2]),
                             op=ALU.mult)
 
@@ -326,38 +341,40 @@ def tile_bcnnresnet_v_kernel(tc, feat, W, b, norm, grad_out, out_0, out_1):
                 PE.matmul(out=tiles["acc", g][:, 128 * t:128 * (t + 1)], lhsT=tt[:, 96 * k:96 * k + 128], rhs=idf[:],
                           start=(k == 0), stop=(k == last - 1), is_transpose=True)
 
-        def back(g):
-            accs = sb.tile([P, 512], F32, name="accs", tag="xd")
-            S.copy(out=accs[:], in_=tiles["acc", g][:])
+        def back(t0, t1):
+            g, n = t0 // 4, t1 - t0
+            accs = sb.tile([P, n, 128], F32, name="accs", tag="xd")
+            S.copy(out=accs[:], in_=tiles["acc", g][:, 128 * (t0 % 4):128 * (t0 % 4 + n)].rearrange("p (t n) -> p t n", n=128))
             bank = zbank(F32, "bb")
-            for t in range(4):
-                PE.transpose(bank[:, 96 * t:96 * t + 128], accs[:, 128 * t:128 * (t + 1)], idf[:])
-            tiles["bb", g] = bank
+            for t in range(n):
+                PE.transpose(bank[:, 96 * t:96 * t + 128], accs[:, t, :], idf[:])
+            tiles["bb", t0] = bank
 
-        def finish(g):
-            bank = tiles["bb", g]
-            sl = slice(4 * D * g, 4 * D * (g + 1))
-            bs = sb.tile([P, 4 * D], F32, name="bs", tag="neg")
+        def finish(t0, t1):
+            g, n = t0 // 4, t1 - t0
+            bank = tiles["bb", t0]
+            sl = slice(D * t0, D * t1)
+            bs = sb.tile([P, n * D], F32, name="bs", tag="neg")
             V.tensor_reduce(out=bs[:].rearrange("p (r e) -> p r e", e=2),
-                            in_=bank[:, 0:384].rearrange("p (r s e) -> p r e s", s=2, e=2), axis=AX.X, op=ALU.add)
-            es = sb.tile([P, 4], F32, name="es", tag="es")
-            V.tensor_reduce(out=es[:], in_=esum[:, 4 * g:4 * g + 4, :], axis=AX.X, op=ALU.add)
-            ab = sb.tile([P, 4, D], F32, name="ab", tag="zd")
+                            in_=bank[:, 0:96 * n].rearrange("p (r s e) -> p r e s", s=2, e=2), axis=AX.X, op=ALU.add)
+            es = sb.tile([P, n], F32, name="es", tag="es")
+            V.tensor_reduce(out=es[:], in_=esum[:, t0:t1, :], axis=AX.X, op=ALU.add)
+            ab = sb.tile([P, n, D], F32, name="ab", tag="zd")
             V.tensor_tensor(out=ab[:].rearrange("p t m -> p (t m)"), in0=bs[:], in1=absf[:, sl], op=ALU.mult)
-            t1 = sb.tile([P, 4 * D], F32, name="t1", tag="f")
-            V.tensor_tensor(out=t1[:], in0=bs[:], in1=tiles["hs"][:, sl], op=ALU.mult)
-            s1 = sb.tile([P, 4], F32, name="s1", tag="s1")
+            t1_ = sb.tile([P, n * D], F32, name="t1", tag="f")
+            V.tensor_tensor(out=t1_[:], in0=bs[:], in1=tiles["hs"][:, sl], op=ALU.mult)
+            s1 = sb.tile([P, n], F32, name="s1", tag="s1")
             V.tensor_reduce(out=s1[:], in_=ab[:], axis=AX.X, op=ALU.add)
-            s2 = sb.tile([P, 4], F32, name="s2", tag="s2")
+            s2 = sb.tile([P, n], F32, name="s2", tag="s2")
             V.scalar_tensor_tensor(out=s2[:], in0=es[:], scalar=2 * EPS, in1=s1[:], op0=ALU.mult, op1=ALU.add)
-            V.tensor_tensor(out=ab[:], in0=tiles["ks"][:, sl].rearrange("p (t m) -> p t m", t=4),
-                            in1=s2[:].unsqueeze(2).to_broadcast([P, 4, D]), op=ALU.mult)
-            res = sb.tile([P, 4, D], F32, name="res", tag="sh")
-            V.tensor_tensor(out=res[:].rearrange("p t m -> p (t m)"), in0=t1[:], in1=ab[:].rearrange("p t m -> p (t m)"), op=ALU.subtract)
-            nc.sync.dma_start(out=out_0[512 * g:512 * (g + 1), :].rearrange("(p t) d -> p t d", t=4), in_=res[:])
+            V.tensor_tensor(out=ab[:], in0=tiles["ks"][:, sl].rearrange("p (t m) -> p t m", t=n),
+                            in1=s2[:].unsqueeze(2).to_broadcast([P, n, D]), op=ALU.mult)
+            res = sb.tile([P, n, D], F32, name="res", tag="sh")
+            V.tensor_tensor(out=res[:].rearrange("p t m -> p (t m)"), in0=t1_[:], in1=ab[:].rearrange("p t m -> p (t m)"), op=ALU.subtract)
+            nc.sync.dma_start(out=out_0[512 * g:512 * (g + 1), :].rearrange("(p t) d -> p t d", t=4)[:, t0 % 4:t0 % 4 + n, :], in_=res[:])
 
         def late_consts():
-            a2s = sb.tile([P, NS, 2], BF16, name="a2s", tag="xd")
+            a2s = sb.tile([P, NS, 2], BF16, name="a2s")
             S.copy(out=a2s[:], in_=absf[:].unsqueeze(2).to_broadcast([P, NS, 2]))
             asum = sb.tile([P, 8], F32, name="asum")
             V.tensor_reduce(out=asum[:], in_=absf[:].rearrange("p (n m) -> p n m", m=D), axis=AX.X, op=ALU.add)
@@ -377,6 +394,7 @@ def tile_bcnnresnet_v_kernel(tc, feat, W, b, norm, grad_out, out_0, out_1):
             G.tensor_tensor(out=ks[:], in0=sgn[:].rearrange("p (n m) -> p n m", m=D),
                             in1=k2[:].unsqueeze(2).to_broadcast([P, 8, D]), op=ALU.mult)
             tiles["a2"] = c2[:, 0:768].rearrange("p (n m s) -> p n m s", n=8, s=2)
+            tiles["a2s"] = a2s[:].rearrange("p (n m) s -> p n m s", n=8)
             tiles["hs"] = hr
             tiles["ks"] = ks[:].rearrange("p n m -> p (n m)")
 
@@ -384,90 +402,110 @@ def tile_bcnnresnet_v_kernel(tc, feat, W, b, norm, grad_out, out_0, out_1):
             tiles["t"] = sb.tile([P, 2, TW], F32, name="t", tag="w1", align_bytes=64)
             G.memset(tiles["t"][:, :, ROWS * 96:TW], 0.0)
 
-        def dw(unit):
-            ct, q = divmod(unit, 5)
-            if ct < 2 and q == 0:
-                tiles["st", ct] = sb.tile([P, DD], F32, name="st%d" % ct, tag="g%d" % ct)[:]
-            if ct == 2 and q == 0:
-                both = sb.tile([P, 2, DD], F32, name="st2", tag="x0", align_bytes=64)
-                tiles["st", 2], tiles["st", 3] = both[:, 0, :], both[:, 1, :]
-            st = tiles["st", ct % 4]
+        def dw(unit, tags):
+            q, ct = divmod(unit, 8)
+            if unit == 0:
+                both = sb.tile([P, 2, 4, 512], F32, name="st0", tag="x0", align_bytes=64)
+                tiles["st", 0], tiles["st", 1] = both[:, 0], both[:, 1]
+            if unit in (8, 12):
+                tiles["st", unit // 4] = sb.tile([P, 4, 512], F32, name="st2", tag="g%d" % (unit // 4 - 2))[:]
+            st = tiles["st", (unit // 4) % 4]
             c0 = min(512 * q, DD - 512)
-            bank = ps.tile([P, 512], F32, name="dwb", tag="dw" if unit % 2 == 0 else "cst")
+            n = c0 + 512 - 512 * q
+            tag = tags[unit % len(tags)]
+            bank = zbank(F32, "dwz") if tag == "z" else ps.tile([P, 512], F32, name="dwb", tag=tag)
             for g in range(2):
                 sl = slice(1024 * g + 128 * ct, 1024 * g + 128 * (ct + 1))
                 PE.matmul_mx(out=bank[:], lhsT=gsc[:, sl].bitcast(E5), lhsT_scale=gss[:, sl], rhs=xc[g][:, c0:c0 + 512].bitcast(E4),
                              rhs_scale=xs[g][:, c0:c0 + 512], start=(g == 0), stop=(g == 1))
-            S.copy(out=st[:, 512 * q:c0 + 512], in_=bank[:, 512 * q - c0:512])
-            if q in (1, 4):
-                lo = 0 if q == 1 else 1024
-                nc.sync.dma_start(out=out_1[128 * ct:128 * (ct + 1), lo:c0 + 512], in_=st[:, lo:c0 + 512])
+            S.copy(out=st[:, ct % 4, 0:n], in_=bank[:, 512 - n:512])
+            if ct % 2 == 1:
+                nc.sync.dma_start(out=out_1[128 * (ct - 1):128 * (ct + 1), 512 * q:512 * q + n].rearrange("(c p) w -> p c w", c=2),
+                                  in_=st[:, ct % 4 - 1:ct % 4 + 1, 0:n])
 
-        Q2G = {(1, c) for c in range(1, 5)}
+        Q2G = {(1, c) for c in range(0, 5)}
         chunks = [(g, c) for g in range(2) for c in range(5)]
-        fills = {0: [lambda: gt_fill(0), lambda: gt_fill(1)],
-                 6: [lambda: gs_fill(0), lambda: gs_fill(1)], 7: [lambda: gs_fill(2), lambda: gs_fill(3)],
-                 8: [lambda: gt_fill(2), lambda: gt_fill(3)]}
-        for n in range(5):
-            fills[1 + n] = [lambda m=m: w_fill(m // 5, m % 5) for m in (2 * n, 2 * n + 1)]
+        wf = [lambda m=m: w_fill(m // 5, m % 5) for m in range(10)]
+        fills = {0: [lambda: gt_fill(0), lambda: gt_fill(1)], 1: wf[0:4], 2: wf[4:8], 3: wf[8:10],
+                 5: [lambda: gs_fill(0), lambda: gs_fill(1), lambda: gs_fill(2), lambda: gs_fill(3)],
+                 6: [lambda: gt_fill(2), lambda: gt_fill(3)]}
         pending = []
+        rows = {}
         fwd_a(0, 0)
+        make_sjn(0)
+        late_consts()
+        fwd_r(0, 0)
         for s in range(11):
             if s + 1 < 10:
                 fwd_a(*chunks[s + 1])
+                if s == 3:
+                    make_sjn(1)
+                fwd_r(*chunks[s + 1])
             if s >= 1:
                 fwd_x(*chunks[s - 1])
             for q in pending:
                 q()
-            if s == 1:
-                late_consts()
-            if s == 6:
+            if s == 4:
                 make_t()
                 dx(0)
-            if s == 7:
+            if s == 6:
                 for q in range(5):
                     x_quant(0, q)
-            pending = [fl_() for fl_ in fills.get(s, [])]
-            if s == 5:
-                mirror(0, range(0, 2))
-            if s == 6:
-                mirror(0, range(2, 7))
+            if s == 7:
+                x_quant(1, 0)
             if s == 9:
-                mirror(1, range(0, 7))
+                x_quant(1, 1)
+            pending = [fl_() for fl_ in fills.get(s, [])]
             if s < 10:
                 fwd_q(*chunks[s])
-            if s in (6, 7, 8, 9):
-                m_pass(s - 6)
-                dx(s - 5)
-                u_pass(s - 6)
-                if s > 6:
-                    t_sum(s - 7, 0, ROWS, ROWS)
-        for q in range(5):
+            if 4 <= s <= 4 + 4:
+                tau = s - 4 - 1
+                if tau >= 0:
+                    m_pass(tau)
+                    if s >= 7:
+                        for u in range(4):
+                            dw(4 * (s - 7) + u, ("dw", "z"))
+                    dx(tau + 1)
+                    u_pass(tau)
+                    rows[tau] = ROWS
+                    if tau > 0:
+                        t_sum(tau - 1, 0, ROWS, ROWS)
+                    if tau == 4:
+                        back(0, 4)
+        t0 = 4
+        unit = 4 * (t0 - 2)
+        m_pass(t0)
+        for q in range(2, 5):
             x_quant(1, q)
-        rows = {3: ROWS}
-        unit = 0
-        for tau in range(4, 8):
-            m_pass(tau)
+        for tau in range(t0, 8):
+            if tau > t0:
+                m_pass(tau)
+            if tau in ():
+                u_pass(tau, G)
+                rows[tau] = ROWS
             n = rows[tau - 1]
             for step in range(3):
-                dw(unit)
-                dw(unit + 1)
                 if tau < 7:
                     dx(tau + 1, (step,))
-                dw(unit + 2)
-                unit = unit + 3
-                if step != 1:
-                    t_sum(tau - 1, 0 if step == 0 else n // 2, n // 2 if step == 0 else n, n)
+                dw(unit, ("dw", "cst"))
+                dw(unit + 1, ("dw", "cst"))
+                unit = unit + 2
+                if step == 2:
+                    t_sum(tau - 1, 0, n, n)
             if tau == 4:
-                back(0)
-            u_pass(tau)
-            rows[tau] = fold(tau, V, fold(tau, V, ROWS))
+                back(0, 4)
+            if tau == 7:
+                back(4, 7)
+            if tau not in ():
+                u_pass(tau)
+                rows[tau] = fold(tau, V if tau == 7 else G, fold(tau, V if tau == 7 else G, ROWS))
             if tau == 5:
-                finish(0)
-        dw(36)
-        dw(37)
+                finish(0, 4)
+        finish(4, 7)
+        for unit in range(unit, 36):
+            dw(unit, ("dw", "cst", "z"))
         t_sum(7, 0, rows[7], rows[7])
-        back(1)
-        dw(38)
-        dw(39)
-        finish(1)
+        back(7, 8)
+        for unit in range(36, 40):
+            dw(unit, ("dw", "cst", "z"))
+        finish(7, 8)

@@ -21,491 +21,434 @@ ACT = mybir.ActivationFunctionType
 AX = mybir.AxisListType
 
 P = 128
-H = 6
-NB = D // H
-RP = H // 2
-CHUNKS = [[0], [1, 6], [2, 5], [3, 4]]
-STEPS = [[0], [1, (0, 2)], [2, (2, 4)], [3, 4], [5, 6, (4, 8)]]
-KC = 126
-KOFF = 4 * KC
-KD = NB * RP * H
-KALL = KOFF + KD
-XW = NB * (H * D + H)
-ROWS = D // 2 + RP
-TW = ROWS * 96 + 32
+N = 512
+TILES = 8
+BAND = 8
+BANDS = D // BAND
+PAIRS = BAND // 2
+BANKS = [[0, 5], [1, 4], [2, 3]]
+KB = PAIRS * (2 * D - BAND * (BANDS - 1))
+KALL = len(BANKS) * KB
+STEPS = [[0], [1], [2], [3], [4, 5]]
+W_PIECES = 2 * len(BANKS)
+W_COLS = W_PIECES * 2 * KB + N - 2 * KB
+ROWS = D // 2
+TERM_COLS = ROWS * 2 * D + P - 2 * D
+X_TILES = 5
+STAGES = 4
+PARKED = [6, 7]
+SCALAR_BANDS = [4, 2]
+EARLY_TILES = {4: 0, 5: 0, 7: 8, 8: 8}
+LATE_UNITS = 5
+LAST_UNITS = 3
 
 
-def width(b):
-    return D - H * (b + 1)
+def width(band):
+    return D - BAND * band
 
 
-def band_start(b):
-    for c, bands in enumerate(CHUNKS):
-        k = KC * c
-        for o in bands:
-            if o == b:
-                return k
-            k = k + RP * width(o)
-    raise ValueError
+def band_start(band):
+    order = [o for bank in BANKS for o in bank]
+    return sum(PAIRS * width(o) for o in order[:order.index(band)])
 
 
 def tile_bcnnresnet_v_kernel(tc, feat, W, b, norm, grad_out, out_0, out_1):
     nc = tc.nc
-    V, S, G, PE = nc.vector, nc.scalar, nc.gpsimd, nc.tensor
-    Q1 = G
+    V, S, PE = nc.vector, nc.scalar, nc.tensor
     with ExitStack() as ctx:
         sb = ctx.enter_context(tc.tile_pool(name="sb", bufs=1))
         ps = ctx.enter_context(tc.psum_pool(name="ps", bufs=1))
+        tiles = {}
+        count = {"bank": 0, "stage": 0, "unit": 0, "rotating": 7}
 
-        def zbank(dtype, name):
-            return ps.tile([P, 512 if dtype == F32 else 1024], dtype, name=name, tag="z", bufs=4)
+        rotation = ["f0", "f1", "f2", "f3", "z0", "z1", "z2"]
+
+        def psum_bank(dtype, name, tag=None):
+            if tag is None:
+                count["bank"] = count["bank"] + 1
+                tag = rotation[count["bank"] % count["rotating"]]
+            return ps.tile([P, N if dtype == F32 else 2 * N], dtype, name=name, tag=tag)
 
         f = sb.tile([P, 2, 4, D], BF16, name="f", tag="f")
         nc.sync.dma_start(out=f[:], in_=feat.rearrange("(g p t) d -> p g t d", g=2, t=4))
         nrm = sb.tile([P, 2, 4], F32, name="nrm")
         nc.sync.dma_start(out=nrm[:], in_=norm.rearrange("(g p t) -> p g t", g=2, t=4))
-        graw = [sb.tile([P, 4, C], BF16, name="graw%d" % g, tag="g%d" % g) for g in range(2)]
-        wraw = [sb.tile([P, 4, DD], BF16, name="wraw%d" % kp, tag="w%d" % kp, align_bytes=64) for kp in range(2)]
-        for dst, src, h in ((graw, grad_out, 0), (wraw, W, 0), (wraw, W, 1), (graw, grad_out, 1)):
-            nc.sync.dma_start(out=dst[h][:], in_=src[512 * h:512 * (h + 1), :].rearrange("(p t) c -> p t c", t=4))
+        g_raw = [sb.tile([P, 4, C], BF16, name="g_raw%d" % g, tag="g%d" % g) for g in range(2)]
+        w_raw = [sb.tile([P, 4, DD], BF16, name="w_raw%d" % kp, tag="w%d" % kp, align_bytes=64) for kp in range(2)]
+        for dst, src, h in ((g_raw, grad_out, 0), (w_raw, W, 0), (w_raw, W, 1), (g_raw, grad_out, 1)):
+            nc.sync.dma_start(out=dst[h][:], in_=src[N * h:N * (h + 1), :].rearrange("(p t) c -> p t c", t=4))
 
-        idb = sb.tile([P, P], BF16, name="idb")
-        make_identity(nc, idb[:])
-        idf = sb.tile([P, P], F32, name="idf")
-        make_identity(nc, idf[:])
+        ident_bf = sb.tile([P, P], BF16, name="ident_bf")
+        make_identity(nc, ident_bf[:])
+        ident_f32 = sb.tile([P, P], F32, name="ident_f32")
+        make_identity(nc, ident_f32[:])
 
-        fl = f[:].rearrange("p g t d -> p (g t d)")
-        NS = 8 * D
-        absf = sb.tile([P, NS], BF16, name="absf")
-        S.activation(out=absf[:], in_=fl, func=ACT.Abs)
-        sgn = sb.tile([P, NS], BF16, name="sgn")
-        S.activation(out=sgn[:], in_=fl, func=ACT.Sign)
-        aj = sb.tile([P, 2, D, 4, 2], BF16, name="aj")
-        S.copy(out=aj[:], in_=absf[:].rearrange("p (g t j) -> p g j t", g=2, t=4).unsqueeze(4).to_broadcast([P, 2, D, 4, 2]))
-        zd = sb.tile([P, NS], BF16, name="zd", tag="zd")
-        V.tensor_scalar(out=zd[:], in0=fl, scalar1=0.0, scalar2=TINY, op0=ALU.is_equal, op1=ALU.mult)
-        rn = sb.tile([P, 8], F32, name="rn")
-        V.reciprocal(out=rn[:], in_=nrm[:].rearrange("p g t -> p (g t)"))
-        amax = sb.tile([P, 2], F32, name="amax")
-        V.tensor_reduce(out=amax[:], in_=absf[:].rearrange("p (g m) -> p g m", g=2), axis=AX.X, op=ALU.max)
-        sh = sb.tile([P, NS], BF16, name="sh", tag="sh")
-        V.tensor_tensor(out=sh[:], in0=sgn[:], in1=zd[:], op=ALU.add)
-        V.tensor_scalar(out=amax[:], in0=amax[:], scalar1=1e-5, scalar2=0.25, op0=ALU.max, op1=ALU.mult)
+        f_flat = f[:].rearrange("p g t d -> p (g t d)")
+        mag = sb.tile([P, TILES * D], BF16, name="mag")
+        S.activation(out=mag[:], in_=f_flat, func=ACT.Abs)
+        mag_row = sb.tile([P, 2, ROWS, 4, 2], BF16, name="mag_row")
+        S.copy(out=mag_row[:], in_=mag[:].rearrange("p (g t r e) -> p g r t e", g=2, t=4, e=2))
+        mag_col = sb.tile([P, 2, D, 4, 2], BF16, name="mag_col")
+        S.copy(out=mag_col[:],
+               in_=mag[:].rearrange("p (g t j) -> p g j t", g=2, t=4).unsqueeze(4).to_broadcast([P, 2, D, 4, 2]))
+        sgn = sb.tile([P, TILES * D], BF16, name="sgn")
+        S.activation(out=sgn[:], in_=f_flat, func=ACT.Sign)
+        tiny_at_0 = sb.tile([P, TILES * D], BF16, name="tiny_at_0", tag="small0")
+        V.tensor_scalar(out=tiny_at_0[:], in0=f_flat, scalar1=0.0, scalar2=TINY, op0=ALU.is_equal, op1=ALU.mult)
+        inv_norm = sb.tile([P, TILES], F32, name="inv_norm")
+        V.reciprocal(out=inv_norm[:], in_=nrm[:].rearrange("p g t -> p (g t)"))
+        top = sb.tile([P, 2], F32, name="top")
+        V.tensor_reduce(out=top[:], in_=mag[:].rearrange("p (g m) -> p g m", g=2), axis=AX.X, op=ALU.max)
+        sgn_tiny = sb.tile([P, TILES * D], BF16, name="sgn_tiny", tag="small1")
+        V.tensor_tensor(out=sgn_tiny[:], in0=sgn[:], in1=tiny_at_0[:], op=ALU.add)
+        V.tensor_scalar(out=top[:], in0=top[:], scalar1=EPS ** 0.5, scalar2=0.25, op0=ALU.max, op1=ALU.mult)
         nu = sb.tile([P, 2], F32, name="nu")
-        V.reciprocal(out=nu[:], in_=amax[:])
+        V.reciprocal(out=nu[:], in_=top[:])
         nu2 = sb.tile([P, 2], F32, name="nu2")
         V.tensor_tensor(out=nu2[:], in0=nu[:], in1=nu[:], op=ALU.mult)
-        rnu = sb.tile([P, 2, 4], F32, name="rnu")
-        V.tensor_tensor(out=rnu[:], in0=rn[:].rearrange("p (g t) -> p g t", g=2), in1=nu[:].unsqueeze(2).to_broadcast([P, 2, 4]), op=ALU.mult)
-        enu = sb.tile([P, 2], F32, name="enu")
-        V.tensor_scalar(out=enu[:], in0=nu2[:], scalar1=EPS, scalar2=None, op0=ALU.mult)
-        cst = ps.tile([P, 1024], BF16, name="cst", tag="cst")
-        ai = cst[:, 0:384].rearrange("p (g r t e) -> p g r t e", g=2, t=4, e=2)
-        si = cst[:, 384:768].rearrange("p (g r t e) -> p g r t e", g=2, t=4, e=2)
-        for src, dst in ((absf, ai), (sh, si)):
-            for g in range(2):
-                PE.matmul(out=dst[:, g], lhsT=idb[:],
-                          rhs=src[:].rearrange("p (g t r e) -> p g r t e", g=2, t=4, e=2)[:, g], start=True, stop=True)
-        sjn = sb.tile([P, 2, D, 4, 2], F32, name="sjn")
+        nu_norm = sb.tile([P, 2, 4], F32, name="nu_norm")
+        V.tensor_tensor(out=nu_norm[:], in0=inv_norm[:].rearrange("p (g t) -> p g t", g=2),
+                        in1=nu[:].unsqueeze(2).to_broadcast([P, 2, 4]), op=ALU.mult)
+        eps_nu2 = sb.tile([P, 2], F32, name="eps_nu2")
+        V.tensor_scalar(out=eps_nu2[:], in0=nu2[:], scalar1=EPS, scalar2=None, op0=ALU.mult)
+        sgn_row = sb.tile([P, 2, ROWS, 4, 2], BF16, name="sgn_row")
+        S.copy(out=sgn_row[:], in_=sgn_tiny[:].rearrange("p (g t r e) -> p g r t e", g=2, t=4, e=2))
+        sgn_col = sb.tile([P, 2, D, 4, 2], F32, name="sgn_col")
 
-        def make_sjn(g):
-            V.tensor_tensor(out=sjn[:, g],
-                            in0=sh[:].rearrange("p (g t j) -> p g j t", g=2, t=4)[:, g].unsqueeze(3).to_broadcast([P, D, 4, 2]),
-                            in1=rnu[:, g].unsqueeze(1).unsqueeze(3).to_broadcast([P, D, 4, 2]), op=ALU.mult)
+        def make_sgn_col(g):
+            V.tensor_tensor(out=sgn_col[:, g],
+                            in0=sgn_tiny[:].rearrange("p (g t j) -> p g j t", g=2, t=4)[:, g].unsqueeze(3)
+                            .to_broadcast([P, D, 4, 2]),
+                            in1=nu_norm[:, g].unsqueeze(1).unsqueeze(3).to_broadcast([P, D, 4, 2]), op=ALU.mult)
 
+        mag32 = sb.tile([P, TILES, D], F32, name="mag32")
+        half_inv_sgn = sb.tile([P, TILES * D], BF16, name="half_inv_sgn")
+        sgn_sum = sb.tile([P, TILES, D], F32, name="sgn_sum")
 
-        sis = sb.tile([P, D // 2, 4, 2], BF16, name="sis")
-        S.copy(out=sis[:], in_=sh[:].rearrange("p (g t r e) -> p g r t e", g=2, t=4, e=2)[:, 1])
-        qq = [sb.tile([P, KALL, 4, 2], F32, name="q%d" % g) for g in range(2)]
-        grp = [sb.tile([P, 2048], BF16, name="grp%d" % i, align_bytes=64) for i in range(4)]
-        wc = [sb.tile([P, 5 * 512], U32, name="wc%d" % i, align_bytes=64) for i in range(2)]
-        ws = [sb.tile([P, 5 * 512], U8, name="ws%d" % i, align_bytes=64) for i in range(2)]
-        gtc = sb.tile([P, 2048], U32, name="gtc", align_bytes=64)
-        gts = sb.tile([P, 2048], U8, name="gts", align_bytes=64)
-        gsc = sb.tile([P, 2048], U32, name="gsc", align_bytes=64)
-        gss = sb.tile([P, 2048], U8, name="gss", align_bytes=64)
-        xc = [sb.tile([P, DD], U32, name="xc%d" % i, align_bytes=64) for i in range(2)]
-        xs = [sb.tile([P, DD], U8, name="xs%d" % i, align_bytes=64) for i in range(2)]
-        esum = sb.tile([P, 8, 3], F32, name="esum")
-        for i in (2, 3):
-            G.memset(grp[i][:].rearrange("p (e k) -> p e k", e=2)[:, :, 4 * 2 * KC:1024], 0.0)
-        state = {"grp": 0}
-        tiles = {}
+        def make_backward_vectors():
+            mag_sum = sb.tile([P, TILES], F32, name="mag_sum")
+            for n in range(TILES):
+                S.activation(out=mag32[:, n, :], in_=mag[:, D * n:D * (n + 1)], func=ACT.Copy, accum_out=mag_sum[:, n:n + 1])
+            big_at_0 = sb.tile([P, TILES * D], BF16, name="big_at_0", tag="small2")
+            V.tensor_scalar(out=big_at_0[:], in0=f_flat, scalar1=0.0, scalar2=0.5 / TINY, op0=ALU.is_equal, op1=ALU.mult)
+            k1 = sb.tile([P, TILES], F32, name="k1")
+            V.scalar_tensor_tensor(out=k1[:], in0=mag_sum[:], scalar=0.5, in1=inv_norm[:], op0=ALU.mult, op1=ALU.mult)
+            V.scalar_tensor_tensor(out=half_inv_sgn[:], in0=sgn[:], scalar=0.5, in1=big_at_0[:], op0=ALU.mult, op1=ALU.add)
+            k2 = sb.tile([P, TILES], F32, name="k2")
+            V.tensor_tensor(out=k2[:], in0=k1[:], in1=inv_norm[:], op=ALU.mult)
+            for n in range(TILES):
+                S.activation(out=sgn_sum[:, n, :], in_=sgn[:, D * n:D * (n + 1)], func=ACT.Copy, scale=k2[:, n:n + 1])
 
-        def next_grp():
-            state["grp"] = state["grp"] + 1
-            return grp[(state["grp"] - 1) % 4]
+        q_all = [sb.tile([P, KALL, 4, 2], F32, name="q%d" % g) for g in range(2)]
+        stages = [sb.tile([P, 4 * N], BF16, name="stage%d" % i, align_bytes=64) for i in range(STAGES)]
+        w_codes = [sb.tile([P, W_COLS], U32, name="w_codes%d" % i, align_bytes=64) for i in range(2)]
+        w_scales = [sb.tile([P, W_COLS], U8, name="w_scales%d" % i, align_bytes=64) for i in range(2)]
+        gc_codes = sb.tile([P, 4 * N], U32, name="gc_codes", align_bytes=64)
+        gc_scales = sb.tile([P, 4 * N], U8, name="gc_scales", align_bytes=64)
+        gs_codes = sb.tile([P, 4 * N], U32, name="gs_codes", align_bytes=64)
+        gs_scales = sb.tile([P, 4 * N], U8, name="gs_scales", align_bytes=64)
+        x_codes = [sb.tile([P, DD], U32, name="x_codes%d" % i, align_bytes=64) for i in range(2)]
+        x_scales = [sb.tile([P, DD], U8, name="x_scales%d" % i, align_bytes=64) for i in range(2)]
+        m_sums = sb.tile([P, TILES, len(BANKS) + BANDS], F32, name="m_sums")
 
-        def quant(src, codes, scales, fmt):
+        def next_stage():
+            count["stage"] = count["stage"] + 1
+            return stages[(count["stage"] - 1) % STAGES]
+
+        def quantise(src, codes, scales, fmt):
             V.quantize_mx(out=codes.bitcast(fmt), scales=scales, in_=src)
 
-        def gt_fill(pair):
-            buf = next_grp()
+        def fill_g_by_class(pair):
+            stage = next_stage()
             for h in range(2):
-                tau = 2 * pair + h
-                words = graw[tau // 4][:, tau % 4, :].bitcast(F32)
-                bank = zbank(F32, "gtb")
+                tile = 2 * pair + h
+                words = g_raw[tile // 4][:, tile % 4, :].bitcast(F32)
+                bank = psum_bank(F32, "gc_bank")
                 for kp in range(2):
                     for u in range(2):
-                        PE.transpose(bank[:, 128 * (2 * kp + u):128 * (2 * kp + u + 1)],
-                                     words[:, 256 * kp + u:256 * (kp + 1):2], idf[:])
-                S.copy(out=buf[:, 1024 * h:1024 * (h + 1)].bitcast(F32).rearrange("p (k n u) -> p k n u", k=2, u=2),
+                        PE.transpose(bank[:, P * (2 * kp + u):P * (2 * kp + u + 1)],
+                                     words[:, 2 * P * kp + u:2 * P * (kp + 1):2], ident_f32[:])
+                S.copy(out=stage[:, 2 * N * h:2 * N * (h + 1)].bitcast(F32).rearrange("p (k n u) -> p k n u", k=2, u=2),
                        in_=bank[:].rearrange("p (k u n) -> p k n u", k=2, u=2))
-            return lambda: quant(buf[:], gtc[:, 512 * pair:512 * (pair + 1)], gts[:, 512 * pair:512 * (pair + 1)], E5)
+            cols = slice(N * pair, N * (pair + 1))
+            return lambda: quantise(stage[:], gc_codes[:, cols], gc_scales[:, cols], E5)
 
-        def gs_fill(piece):
+        def fill_g_by_sample(piece):
             g, half = divmod(piece, 2)
-            buf = next_grp()
+            stage = next_stage()
+            if g == 0:
+                S.copy(out=stage[:].rearrange("p (c i t) -> p c t i", i=4, t=4),
+                       in_=g_raw[g][:, :, N * half:N * (half + 1)].rearrange("p t (c i) -> p c t i", i=4))
+            else:
+                for h in range(2):
+                    bank = psum_bank(BF16, "gs_bank")
+                    for m in range(2):
+                        c0 = N * half + 2 * P * h + P * m
+                        PE.matmul(out=bank[:, N * m:N * (m + 1)].rearrange("p (c t) -> p c t", t=4), lhsT=ident_bf[:],
+                                  rhs=g_raw[g][:, :, c0:c0 + P].rearrange("p t c -> p c t"), start=True, stop=True)
+                    S.copy(out=stage[:, 2 * N * h:2 * N * (h + 1)].bitcast(F32), in_=bank[:].bitcast(F32))
+            cols = slice(N * piece, N * (piece + 1))
+            return lambda: quantise(stage[:], gs_codes[:, cols], gs_scales[:, cols], E5)
+
+        def fill_w(kp, piece):
+            stage = next_stage()
+            by_pair = w_raw[kp][:].rearrange("p t (r e j) -> p r e j t", e=2, j=D)
+            mirrored = w_raw[kp][:].rearrange("p t (j i) -> p j i t", i=D)
+            halves = stage[:, 0:8 * KB].rearrange("p (e k t) -> p e k t", e=2, t=4)
+            bk, half = piece % len(BANKS), KB // 2
             for h in range(2):
-                bank = zbank(BF16, "gsb")
-                for m in range(2):
-                    c0 = 512 * half + 256 * h + 128 * m
-                    PE.matmul(out=bank[:, 512 * m:512 * (m + 1)].rearrange("p (c t) -> p c t", t=4), lhsT=idb[:],
-                              rhs=graw[g][:, :, c0:c0 + 128].rearrange("p t c -> p c t"), start=True, stop=True)
-                S.copy(out=buf[:, 1024 * h:1024 * (h + 1)].bitcast(F32), in_=bank[:].bitcast(F32))
-            return lambda: quant(buf[:], gsc[:, 512 * piece:512 * (piece + 1)], gss[:, 512 * piece:512 * (piece + 1)], E5)
-
-        def w_fill(kp, piece):
-            buf = next_grp()
-            w4 = wraw[kp][:].rearrange("p t (r e j) -> p r e j t", e=2, j=D)
-            wt = wraw[kp][:].rearrange("p t (j i) -> p j i t", i=D)
-            halves = buf[:].rearrange("p (e k t) -> p e k t", e=2, t=4)
-            for h in range(2):
-                bank = zbank(BF16, "wb")
-                if piece < 2:
-                    view = bank[:].rearrange("p (e k t) -> p e k t", e=2, t=4)
-                    for bd in CHUNKS[2 * piece + h]:
-                        k0, w = band_start(bd) % KC, width(bd)
-                        for e in range(2):
-                            PE.matmul(out=view[:, e, k0:k0 + RP * w, :].rearrange("p (r j) t -> p r j t", r=RP), lhsT=idb[:],
-                                      rhs=w4[:, RP * bd:RP * bd + RP, e, D - w:D, :], start=True, stop=True)
-                    S.copy(out=halves[:, :, KC * h:KC * (h + 1), :].bitcast(F32), in_=view[:, :, 0:KC, :].bitcast(F32))
-                elif piece < 4:
-                    view = bank[:].rearrange("p (k e t) -> p k e t", e=2, t=4)
-                    for bd in CHUNKS[2 * (piece - 2) + h]:
-                        k0, w = band_start(bd) % KC, width(bd)
-                        for r in range(RP):
-                            i0 = H * bd + 2 * r
-                            PE.matmul(out=view[:, k0 + r * w:k0 + (r + 1) * w], lhsT=idb[:],
-                                      rhs=wt[:, D - w:D, i0:i0 + 2, :], start=True, stop=True)
-                    S.copy(out=halves[:, :, KC * h:KC * (h + 1), :].bitcast(F32), in_=view[:, 0:KC].bitcast(F32).rearrange("p k e t -> p e k t"))
+                bank = psum_bank(BF16, "w_bank")
+                if piece < len(BANKS):
+                    view = bank[:, 0:4 * KB].rearrange("p (k t) -> p k t", t=4)
+                    for band in BANKS[bk]:
+                        k0, w = band_start(band) - KB * bk, width(band)
+                        for r in range(0, PAIRS, 2):
+                            PE.matmul(out=view[:, k0 + r * w:k0 + (r + 2) * w, :].rearrange("p (r j) t -> p r j t", r=2),
+                                      lhsT=ident_bf[:], rhs=by_pair[:, PAIRS * band + r:PAIRS * band + r + 2, h, D - w:D, :],
+                                      start=True, stop=True)
+                    S.copy(out=halves[:, h].bitcast(F32), in_=view.bitcast(F32))
                 else:
-                    view = bank[:, 0:4 * KD].rearrange("p (b r j t) -> p b r j t", b=NB, r=RP, t=4)
-                    for bd in range(NB):
-                        PE.matmul(out=view[:, bd], lhsT=idb[:],
-                                  rhs=w4[:, RP * bd:RP * bd + RP, h, H * bd:H * bd + H, :], start=True, stop=True)
-                    S.copy(out=buf[:, 1024 * h:1024 * h + 4 * KD].bitcast(F32), in_=bank[:, 0:4 * KD].bitcast(F32))
-            cols = slice(512 * piece, 512 * (piece + 1))
-            return lambda: quant(buf[:], wc[kp][:, cols], ws[kp][:, cols], E4)
+                    view = bank[:, 0:4 * KB].rearrange("p (k e t) -> p k e t", e=2, t=4)
+                    for band in BANKS[bk]:
+                        w = width(band)
+                        for r in range(PAIRS):
+                            k0 = band_start(band) - KB * bk + r * w - half * h
+                            lo, hi = max(k0, 0), min(k0 + w, half)
+                            i0 = BAND * band + 2 * r
+                            if lo < hi:
+                                PE.matmul(out=view[:, lo:hi], lhsT=ident_bf[:],
+                                          rhs=mirrored[:, D - w + lo - k0:D - w + hi - k0, i0:i0 + 2, :], start=True, stop=True)
+                    S.copy(out=halves[:, :, half * h:half * (h + 1), :].bitcast(F32),
+                           in_=view.bitcast(F32).rearrange("p k e t -> p e k t"))
+            cols = slice(2 * KB * piece, 2 * KB * piece + N)
+            return lambda: quantise(stage[:], w_codes[kp][:, cols], w_scales[kp][:, cols], E4)
 
-        def size(part):
-            return RP * width(part) if isinstance(part, int) else RP * H * (part[1] - part[0])
+        def shaped(ap, band, k0):
+            return ap[:, k0:k0 + PAIRS * width(band)].rearrange("p (r j) t e -> p r j t e", r=PAIRS)
 
-        def shaped(ap, part, k0):
-            if isinstance(part, int):
-                return ap[:, k0:k0 + size(part)].rearrange("p (r j) t e -> p r j t e", r=RP)
-            return ap[:, k0:k0 + size(part)].rearrange("p (b r j) t e -> p b r j t e", r=RP, j=H)
+        def step_bands(step):
+            return [(band, sum(PAIRS * width(o) for o in STEPS[step][:n])) for n, band in enumerate(STEPS[step])]
 
-        def q_start(part):
-            return band_start(part) if isinstance(part, int) else KOFF + RP * H * part[0]
+        def by_row(vec, band):
+            return vec[:, PAIRS * band:PAIRS * (band + 1)].unsqueeze(2).to_broadcast([P, PAIRS, width(band), 4, 2])
 
-        def a_parts(c):
-            starts = [sum(size(o) for o in STEPS[c][:n]) for n in range(len(STEPS[c]))]
-            return list(zip(STEPS[c], starts))
+        def by_col(vec, band):
+            return vec[:, D - width(band):D].unsqueeze(1).to_broadcast([P, PAIRS, width(band), 4, 2])
 
-        def by_row(vec, part):
-            if isinstance(part, int):
-                return vec[:, RP * part:RP * part + RP].unsqueeze(2).to_broadcast([P, RP, width(part), 4, 2])
-            return (vec.rearrange("p (b r) t e -> p b r t e", r=RP)[:, part[0]:part[1]].unsqueeze(3)
-                    .to_broadcast([P, part[1] - part[0], RP, H, 4, 2]))
+        def forward_root(g, step):
+            prod = sb.tile([P, PAIRS * D, 4, 2], F32, name="prod", tag="prod", bufs=2)
+            tiles["prod", g, step] = prod
+            for band, k0 in step_bands(step):
+                V.tensor_tensor(out=shaped(prod, band, k0), in0=by_col(mag_col[:, g], band), in1=by_row(mag_row[:, g], band),
+                                op=ALU.mult)
+            for band, k0 in step_bands(step):
+                S.activation(out=shaped(q_all[g], band, band_start(band)), in_=shaped(prod, band, k0),
+                             func=ACT.Abs_reciprocal_sqrt, bias=eps_nu2[:, g:g + 1], scale=nu2[:, g:g + 1])
 
-        def by_col(vec, part):
-            if isinstance(part, int):
-                return vec[:, D - width(part):D].unsqueeze(1).to_broadcast([P, RP, width(part), 4, 2])
-            return (vec.rearrange("p (b j) t e -> p b j t e", j=H)[:, part[0]:part[1]].unsqueeze(2)
-                    .to_broadcast([P, part[1] - part[0], RP, H, 4, 2]))
+        def forward_sign(g, step, factor):
+            for band in STEPS[step]:
+                q = shaped(q_all[g], band, band_start(band))
+                V.tensor_tensor(out=q, in0=q, in1=factor(band), op=ALU.mult)
 
-        def fwd_a(g, c):
-            a = sb.tile([P, KD, 4, 2], F32, name="a", tag="a", bufs=3)
-            tiles["a", g, c] = a
-            for part, k0 in a_parts(c):
-                V.tensor_tensor(out=shaped(a, part, k0), in0=by_row(ai[:, g], part), in1=by_col(aj[:, g], part), op=ALU.mult)
+        def forward_x(g, step):
+            if step == 0:
+                tiles["x", g] = sb.tile([P, DD, 4], BF16, name="x%d" % g, tag=("x0", "w0")[g], align_bytes=64)
+            by_pair = tiles["x", g][:].rearrange("p (r e j) t -> p r e j t", e=2, j=D)
+            square = tiles["x", g][:].rearrange("p (i j) t -> p i j t", j=D)
+            for band, k0 in step_bands(step):
+                prod, q = shaped(tiles["prod", g, step], band, k0), shaped(q_all[g], band, band_start(band))
+                i0, i1 = BAND * band, BAND * (band + 1)
+                for e in range(2):
+                    V.scalar_tensor_tensor(out=by_pair[:, PAIRS * band:PAIRS * (band + 1), e, i0:D, :], in0=prod[:, :, :, :, e],
+                                           scalar=EPS, in1=q[:, :, :, :, e], op0=ALU.add, op1=ALU.mult)
+                if i1 < D:
+                    S.copy(out=square[:, i1:D, i0:i1, :], in_=square[:, i0:i1, i1:D, :].rearrange("p i j t -> p j i t"))
 
-        def fwd_r(g, c):
-            a = tiles["a", g, c]
-            for part, k0 in a_parts(c):
-                S.activation(out=qq[g][:, q_start(part):q_start(part) + size(part)], in_=a[:, k0:k0 + size(part)],
-                             func=ACT.Abs_reciprocal_sqrt, bias=enu[:, g:g + 1], scale=nu2[:, g:g + 1])
-            for part in STEPS[c]:
-                q = shaped(qq[g], part, q_start(part))
-                G.tensor_tensor(out=q, in0=q, in1=by_col(sjn[:, g], part), op=ALU.mult)
+        def quantise_x(g, xt):
+            cols = slice(N * xt, min(N * (xt + 1), DD))
+            quantise(tiles["x", g][:, cols, :].rearrange("p c t -> p (c t)"), x_codes[g][:, cols], x_scales[g][:, cols], E4)
 
-        def fwd_q(g, c):
-            for part in STEPS[c]:
-                q = shaped(qq[g], part, q_start(part))
-                if (g, c) in Q2G:
-                    G.tensor_tensor(out=q, in0=q, in1=by_row(sis[:], part), op=ALU.mult)
-                else:
-                    V.tensor_tensor(out=q, in0=by_row(si[:, g], part), in1=q, op=ALU.mult)
+        def dx_bank(tile, bk):
+            bank = psum_bank(F32, "dx_bank", None if tile in PARKED else "z%d" % bk)
+            passes = [(kp, piece) for piece in (bk, bk + len(BANKS)) for kp in range(2)]
+            for n, (kp, piece) in enumerate(passes):
+                samples = slice(2 * P * tile + P * kp, 2 * P * tile + P * (kp + 1))
+                cols = slice(2 * KB * piece, 2 * KB * piece + N)
+                PE.matmul_mx(out=bank[:], lhsT=gc_codes[:, samples].bitcast(E5), lhsT_scale=gc_scales[:, samples],
+                             rhs=w_codes[kp][:, cols].bitcast(E4), rhs_scale=w_scales[kp][:, cols],
+                             start=(n == 0), stop=(n == len(passes) - 1))
+            tiles["dx", tile, bk] = bank[:, 0:2 * KB].rearrange("p (e k) -> p k e", e=2)
 
-        def fwd_x(g, c):
-            if ("x", g) not in tiles:
-                tiles["x", g] = sb.tile([P, XW, 4], BF16, name="x%d" % g, tag="x0" if g == 0 else "w0", align_bytes=64)
-            x = tiles["x", g]
-            a = tiles["a", g, c]
-            x4 = x[:, 0:DD, :].rearrange("p (r e j) t -> p r e j t", e=2, j=D)
-            skew = x[:].rearrange("p (b y) t -> p b y t", b=NB)[:, :, 0:H * D, :].rearrange("p b (r e j) t -> p e b r j t", r=RP, e=2)
-            for part, k0 in a_parts(c):
-                pa, pq = shaped(a, part, k0), shaped(qq[g], part, q_start(part))
-                if isinstance(part, int):
-                    for e in range(2):
-                        V.scalar_tensor_tensor(out=x4[:, RP * part:RP * part + RP, e, D - width(part):D, :], in0=pa[:, :, :, :, e],
-                                               scalar=EPS, in1=pq[:, :, :, :, e], op0=ALU.add, op1=ALU.mult)
-                    mirror(g, [part])
-                else:
-                    xd = sb.tile([P, 2, part[1] - part[0], RP, H, 4], BF16, name="xd", tag="xd")
-                    for e in range(2):
-                        V.scalar_tensor_tensor(out=xd[:, e], in0=pa[:, :, :, :, :, e], scalar=EPS, in1=pq[:, :, :, :, :, e],
-                                               op0=ALU.add, op1=ALU.mult)
-                    for e in range(2):
-                        S.copy(out=skew[:, e, part[0]:part[1], :, 0:H, :], in_=xd[:, e])
+        def park_dx(tile):
+            parked = sb.tile([P, KALL, 2], F32, name="parked", tag="g%d" % PARKED.index(tile))
+            for bk in range(len(BANKS)):
+                dx_bank(tile, bk)
+                S.copy(out=parked[:, KB * bk:KB * (bk + 1), :], in_=tiles["dx", tile, bk])
+                tiles["dx", tile, bk] = parked[:, KB * bk:KB * (bk + 1), :]
 
-        def mirror(g, bands):
-            xn = tiles["x", g][:, 0:DD, :].rearrange("p (i j) t -> p i j t", j=D)
-            for bd in bands:
-                w = width(bd)
-                S.copy(out=xn[:, D - w:D, H * bd:H * bd + H, :], in_=xn[:, H * bd:H * bd + H, D - w:D, :].rearrange("p i j t -> p j i t"))
-
-        def x_quant(g, q):
-            n = 512 if q < 4 else 256
-            quant(tiles["x", g][:, 512 * q:512 * q + n, :].rearrange("p c t -> p (c t)"),
-                  xc[g][:, 512 * q:512 * q + n], xs[g][:, 512 * q:512 * q + n], E4)
-
-        def dx(tau, bks=(0, 1, 2)):
-            banks = tiles.setdefault(("z", tau), [])
-            for bk in bks:
-                bank = zbank(F32, "zb")
-                passes = [(kp, pc) for pc in ((bk, bk + 2) if bk < 2 else (4,)) for kp in range(2)]
-                for n, (kp, pc) in enumerate(passes):
-                    st = slice(256 * tau + 128 * kp, 256 * tau + 128 * (kp + 1))
-                    mv = slice(512 * pc, 512 * (pc + 1))
-                    PE.matmul_mx(out=bank[:], lhsT=gtc[:, st].bitcast(E5), lhsT_scale=gts[:, st], rhs=wc[kp][:, mv].bitcast(E4),
-                                 rhs_scale=ws[kp][:, mv], start=(n == 0), stop=(n == len(passes) - 1))
-                banks.append(bank)
-
-        def m_pass(tau):
-            g, t = divmod(tau, 4)
+        def make_terms(tile):
+            g, t = divmod(tile, 4)
             m = sb.tile([P, KALL, 2], F32, name="m", tag="m", bufs=2)
-            tiles["m", tau] = m
-            for bk, bank in enumerate(tiles["z", tau]):
-                k0, n = 2 * KC * bk, (2 * KC if bk < 2 else KD)
-                V.scalar_tensor_tensor(out=m[:, k0:k0 + n, :], in0=bank[:].rearrange("p (e k) -> p k e", e=2)[:, 0:n, :], scalar=1.0,
-                                       in1=qq[g][:, k0:k0 + n, t, :], op0=ALU.mult, op1=ALU.mult, accum_out=esum[:, tau, bk:bk + 1])
+            for bk in range(len(BANKS)):
+                ks = slice(KB * bk, KB * (bk + 1))
+                V.scalar_tensor_tensor(out=m[:, ks, :], in0=tiles["dx", tile, bk], scalar=1.0, in1=q_all[g][:, ks, t, :],
+                                       op0=ALU.mult, op1=ALU.mult, accum_out=m_sums[:, tile, bk:bk + 1])
+            rows = tiles["terms"][:, tile % 2, 0:ROWS * 2 * D].rearrange("p (r s m) -> p r s m", s=2, m=D)
+            a = mag32[:, tile]
+            for band in [o for bank in BANKS for o in bank]:
+                w, k0, r0, i0 = width(band), band_start(band), PAIRS * band, BAND * band
+                mb = m[:, k0:k0 + PAIRS * w, :].rearrange("p (r j) e -> p r j e", r=PAIRS)
+                if band < SCALAR_BANDS[g]:
+                    for i in range(BAND):
+                        S.activation(out=rows[:, r0 + i // 2, i % 2, i0:D], in_=mb[:, i // 2, :, i % 2], func=ACT.Copy,
+                                     scale=a[:, i0 + i:i0 + i + 1])
+                else:
+                    V.tensor_tensor(out=rows[:, r0:r0 + PAIRS, :, i0:D], in0=mb.rearrange("p r j e -> p r e j"),
+                                    in1=a[:, i0:i0 + BAND].rearrange("p (r e) -> p r e", e=2).unsqueeze(3)
+                                    .to_broadcast([P, PAIRS, 2, w]), op=ALU.mult)
+                if w > BAND:
+                    below = rows[:, r0 + PAIRS:ROWS].rearrange("p r s m -> p (r s) m")[:, :, i0:i0 + BAND]
+                    V.tensor_tensor(out=below.rearrange("p j (r e) -> p j r e", e=2),
+                                    in0=mb[:, :, BAND:w, :].rearrange("p r j e -> p j r e"),
+                                    in1=a[:, i0 + BAND:D].unsqueeze(2).unsqueeze(3).to_broadcast([P, w - BAND, PAIRS, 2]),
+                                    op=ALU.mult)
+                unread = sb.tile([P, PAIRS, BAND, 2], F32, name="unread", tag="unread")
+                S.activation(out=unread[:], in_=mb[:, :, 0:BAND, :], func=ACT.Copy, scale=-0.5,
+                             accum_out=m_sums[:, tile, len(BANKS) + band:len(BANKS) + band + 1])
 
-        def u_pass(tau, E=V):
-            m = tiles["m", tau]
-            tt = tiles["t"][:, tau % 2, :]
-            a2 = tiles["a2" if E is V else "a2s"][:, tau]
-            rows = tt[:, 0:ROWS * 96].rearrange("p (k R e s) -> p k R e s", R=D // 2, e=2, s=2)
-            for bd in [o for c in CHUNKS for o in c]:
-                w, k0, r0 = width(bd), band_start(bd), RP * bd
-                mb = m[:, k0:k0 + RP * w, :].rearrange("p (r jp jj) e -> p r jp jj e", r=RP, jj=2)
-                E.tensor_tensor(out=rows[:, r0:r0 + RP, r0 + RP:D // 2], in0=mb.rearrange("p r jp jj e -> p r jp e jj"),
-                                in1=a2[:, 2 * r0:2 * r0 + H, :].rearrange("p (r e) s -> p r e s", e=2).unsqueeze(2)
-                                .to_broadcast([P, RP, w // 2, 2, 2]), op=ALU.mult)
-                E.tensor_tensor(out=rows[:, r0 + RP:D // 2, r0:r0 + RP].rearrange("p jp r jj e -> p r jp jj e"), in0=mb,
-                                in1=a2[:, D - w:D, :].rearrange("p (jp jj) s -> p jp jj s", jj=2).unsqueeze(1)
-                                .to_broadcast([P, RP, w // 2, 2, 2]), op=ALU.mult)
-            md = m[:, KOFF:KALL, :].rearrange("p (b r jp jj) e -> p b r jp jj e", b=NB, r=RP, jj=2)
-            skew = tt[:, 0:NB * 300].rearrange("p (b y) -> p b y", b=NB)[:, :, 0:288].rearrange("p b (r y) -> p b r y", r=RP)[:, :, :, 0:12]
-            E.tensor_tensor(out=skew.rearrange("p b r (jp e jj) -> p b r jp e jj", e=2, jj=2), in0=md.rearrange("p b r jp jj e -> p b r jp e jj"),
-                            in1=a2.rearrange("p (b r e) s -> p b r e s", r=RP, e=2).unsqueeze(3).to_broadcast([P, NB, RP, RP, 2, 2]),
-                            op=ALU.mult)
-            E.tensor_tensor(out=rows[:, D // 2:ROWS].rearrange("p jp (b r) jj e -> p b r jp jj e", r=RP), in0=md,
-                            in1=a2.rearrange("p (b jp jj) s -> p b jp jj s", jp=RP, jj=2).unsqueeze(2).to_broadcast([P, NB, RP, RP, 2, 2]),
-                            op=ALU.mult)
+        def fold_terms(tile):
+            terms = tiles["terms"][:, tile % 2, :]
+            rows = ROWS
+            for n in range(tile // 4 + tile // (TILES - 1)):
+                rows = rows // 2
+                V.tensor_tensor(out=terms[:, 0:2 * D * rows], in0=terms[:, 0:2 * D * rows],
+                                in1=terms[:, 2 * D * rows:4 * D * rows], op=ALU.add)
+            tiles["rows", tile] = rows
 
-        def fold(tau, eng, n_from):
-            tt = tiles["t"][:, tau % 2, :]
-            n_to = (n_from + 1) // 2
-            k = n_from - n_to
-            eng.tensor_tensor(out=tt[:, 0:96 * k], in0=tt[:, 0:96 * k], in1=tt[:, 96 * n_to:96 * n_from], op=ALU.add)
-            return n_to
+        def sum_terms(tile):
+            g, t = divmod(tile, 4)
+            if t == 0:
+                tiles["acc", g] = psum_bank(F32, "acc", "acc")
+            terms, rows = tiles["terms"][:, tile % 2, :], tiles["rows", tile]
+            for r in range(rows):
+                PE.matmul(out=tiles["acc", g][:, P * t:P * (t + 1)], lhsT=terms[:, 2 * D * r:2 * D * r + P], rhs=ident_f32[:],
+                          start=(r == 0), stop=(r == rows - 1), is_transpose=True)
 
-        def t_sum(tau, lo, hi, last):
-            g, t = divmod(tau, 4)
-            if ("acc", g) not in tiles:
-                tiles["acc", g] = ps.tile([P, 512], F32, name="acc", tag="acc")
-            tt = tiles["t"][:, tau % 2, :]
-            for k in range(lo, hi):
-                PE.matmul(out=tiles["acc", g][:, 128 * t:128 * (t + 1)], lhsT=tt[:, 96 * k:96 * k + 128], rhs=idf[:],
-                          start=(k == 0), stop=(k == last - 1), is_transpose=True)
-
-        def back(t0, t1):
-            g, n = t0 // 4, t1 - t0
-            accs = sb.tile([P, n, 128], F32, name="accs", tag="xd")
-            S.copy(out=accs[:], in_=tiles["acc", g][:, 128 * (t0 % 4):128 * (t0 % 4 + n)].rearrange("p (t n) -> p t n", n=128))
-            bank = zbank(F32, "bb")
+        def turn_back(t0, t1):
+            n = t1 - t0
+            sums = sb.tile([P, n, P], F32, name="sums", tag="sums")
+            S.copy(out=sums[:], in_=tiles["acc", t0 // 4][:, P * (t0 % 4):P * (t0 % 4 + n)].rearrange("p (t n) -> p t n", n=P))
+            bank = psum_bank(F32, "back")
             for t in range(n):
-                PE.transpose(bank[:, 96 * t:96 * t + 128], accs[:, t, :], idf[:])
-            tiles["bb", t0] = bank
+                PE.transpose(bank[:, 2 * D * t:2 * D * t + P], sums[:, t, :], ident_f32[:])
+            tiles["back", t0] = bank
 
         def finish(t0, t1):
             g, n = t0 // 4, t1 - t0
-            bank = tiles["bb", t0]
-            sl = slice(D * t0, D * t1)
-            bs = sb.tile([P, n * D], F32, name="bs", tag="neg")
-            V.tensor_reduce(out=bs[:].rearrange("p (r e) -> p r e", e=2),
-                            in_=bank[:, 0:96 * n].rearrange("p (r s e) -> p r e s", s=2, e=2), axis=AX.X, op=ALU.add)
-            es = sb.tile([P, n], F32, name="es", tag="es")
-            V.tensor_reduce(out=es[:], in_=esum[:, t0:t1, :], axis=AX.X, op=ALU.add)
-            ab = sb.tile([P, n, D], F32, name="ab", tag="zd")
-            V.tensor_tensor(out=ab[:].rearrange("p t m -> p (t m)"), in0=bs[:], in1=absf[:, sl], op=ALU.mult)
-            t1_ = sb.tile([P, n * D], F32, name="t1", tag="f")
-            V.tensor_tensor(out=t1_[:], in0=bs[:], in1=tiles["hs"][:, sl], op=ALU.mult)
-            s1 = sb.tile([P, n], F32, name="s1", tag="s1")
-            V.tensor_reduce(out=s1[:], in_=ab[:], axis=AX.X, op=ALU.add)
-            s2 = sb.tile([P, n], F32, name="s2", tag="s2")
-            V.scalar_tensor_tensor(out=s2[:], in0=es[:], scalar=2 * EPS, in1=s1[:], op0=ALU.mult, op1=ALU.add)
-            V.tensor_tensor(out=ab[:], in0=tiles["ks"][:, sl].rearrange("p (t m) -> p t m", t=n),
-                            in1=s2[:].unsqueeze(2).to_broadcast([P, n, D]), op=ALU.mult)
-            res = sb.tile([P, n, D], F32, name="res", tag="sh")
-            V.tensor_tensor(out=res[:].rearrange("p t m -> p (t m)"), in0=t1_[:], in1=ab[:].rearrange("p t m -> p (t m)"), op=ALU.subtract)
-            nc.sync.dma_start(out=out_0[512 * g:512 * (g + 1), :].rearrange("(p t) d -> p t d", t=4)[:, t0 % 4:t0 % 4 + n, :], in_=res[:])
+            cols = slice(D * t0, D * t1)
+            b_sum = sb.tile([P, n * D], F32, name="b_sum", tag="small2")
+            V.tensor_reduce(out=b_sum[:].rearrange("p (t m) -> p t m", m=D),
+                            in_=tiles["back", t0][:, 0:2 * D * n].rearrange("p (t s m) -> p t m s", s=2, m=D),
+                            axis=AX.X, op=ALU.add)
+            m_half = sb.tile([P, n], F32, name="m_half", tag="m_half")
+            V.tensor_reduce(out=m_half[:], in_=m_sums[:, t0:t1, :], axis=AX.X, op=ALU.add)
+            ab = sb.tile([P, n, D], F32, name="ab", tag="small0")
+            V.tensor_tensor(out=ab[:].rearrange("p t m -> p (t m)"), in0=b_sum[:], in1=mag[:, cols], op=ALU.mult)
+            first = sb.tile([P, n * D], F32, name="first", tag="f")
+            V.tensor_tensor(out=first[:], in0=b_sum[:], in1=half_inv_sgn[:, cols], op=ALU.mult)
+            ab_sum = sb.tile([P, n], F32, name="ab_sum", tag="ab_sum")
+            V.tensor_reduce(out=ab_sum[:], in_=ab[:], axis=AX.X, op=ALU.add)
+            dot2 = sb.tile([P, n], F32, name="dot2", tag="dot2")
+            V.scalar_tensor_tensor(out=dot2[:], in0=m_half[:], scalar=2 * EPS, in1=ab_sum[:], op0=ALU.mult, op1=ALU.add)
+            V.tensor_tensor(out=ab[:], in0=sgn_sum[:, t0:t1, :], in1=dot2[:].unsqueeze(2).to_broadcast([P, n, D]), op=ALU.mult)
+            res = sb.tile([P, n, D], F32, name="res", tag="small1" if t1 < TILES else "res")
+            V.tensor_tensor(out=res[:].rearrange("p t m -> p (t m)"), in0=first[:], in1=ab[:].rearrange("p t m -> p (t m)"),
+                            op=ALU.subtract)
+            nc.sync.dma_start(out=out_0[N * g:N * (g + 1), :].rearrange("(p t) d -> p t d", t=4)[:, t0 % 4:t0 % 4 + n, :],
+                              in_=res[:])
 
-        def late_consts():
-            a2s = sb.tile([P, NS, 2], BF16, name="a2s")
-            S.copy(out=a2s[:], in_=absf[:].unsqueeze(2).to_broadcast([P, NS, 2]))
-            asum = sb.tile([P, 8], F32, name="asum")
-            V.tensor_reduce(out=asum[:], in_=absf[:].rearrange("p (n m) -> p n m", m=D), axis=AX.X, op=ALU.add)
-            hr = sb.tile([P, NS], BF16, name="hr")
-            h0 = sb.tile([P, NS], BF16, name="h0", tag="neg")
-            V.tensor_scalar(out=h0[:], in0=fl, scalar1=0.0, scalar2=0.5 / TINY, op0=ALU.is_equal, op1=ALU.mult)
-            k1 = sb.tile([P, 8], F32, name="k1")
-            V.scalar_tensor_tensor(out=k1[:], in0=asum[:], scalar=0.5, in1=rn[:], op0=ALU.mult, op1=ALU.mult)
-            V.scalar_tensor_tensor(out=hr[:], in0=sgn[:], scalar=0.5, in1=h0[:], op0=ALU.mult, op1=ALU.add)
-            k2 = sb.tile([P, 8], F32, name="k2")
-            V.tensor_tensor(out=k2[:], in0=k1[:], in1=rn[:], op=ALU.mult)
-            c2 = ps.tile([P, 1024], BF16, name="c2", tag="c2")
-            for h in range(2):
-                PE.matmul(out=c2[:, 384 * h:384 * (h + 1)], lhsT=idb[:],
-                          rhs=a2s[:].rearrange("p m s -> p (m s)")[:, 384 * h:384 * (h + 1)], start=True, stop=True)
-            ks = sb.tile([P, 8, D], F32, name="ks")
-            G.tensor_tensor(out=ks[:], in0=sgn[:].rearrange("p (n m) -> p n m", m=D),
-                            in1=k2[:].unsqueeze(2).to_broadcast([P, 8, D]), op=ALU.mult)
-            tiles["a2"] = c2[:, 0:768].rearrange("p (n m s) -> p n m s", n=8, s=2)
-            tiles["a2s"] = a2s[:].rearrange("p (n m) s -> p n m s", n=8)
-            tiles["hs"] = hr
-            tiles["ks"] = ks[:].rearrange("p n m -> p (n m)")
+        def dw_units(n):
+            for unit in range(count["unit"], count["unit"] + n):
+                xt, ct = divmod(unit, C // P)
+                if unit == 0:
+                    tiles["out"] = sb.tile([P, C // P, N], F32, name="out", tag="x0", align_bytes=64)
+                c0 = min(N * xt, DD - N)
+                new = c0 + N - N * xt
+                bank = psum_bank(F32, "dw_bank")
+                for g in range(2):
+                    classes = slice(C * g + P * ct, C * g + P * (ct + 1))
+                    PE.matmul_mx(out=bank[:], lhsT=gs_codes[:, classes].bitcast(E5), lhsT_scale=gs_scales[:, classes],
+                                 rhs=x_codes[g][:, c0:c0 + N].bitcast(E4), rhs_scale=x_scales[g][:, c0:c0 + N],
+                                 start=(g == 0), stop=(g == 1))
+                S.copy(out=tiles["out"][:, ct, 0:new], in_=bank[:, N - new:N])
+                if ct % 2 == 1:
+                    nc.sync.dma_start(out=out_1[P * (ct - 1):P * (ct + 1), N * xt:N * xt + new].rearrange("(c p) w -> p c w", c=2),
+                                      in_=tiles["out"][:, ct - 1:ct + 1, 0:new])
+            count["unit"] = count["unit"] + n
 
-        def make_t():
-            tiles["t"] = sb.tile([P, 2, TW], F32, name="t", tag="w1", align_bytes=64)
-            G.memset(tiles["t"][:, :, ROWS * 96:TW], 0.0)
-
-        def dw(unit, tags):
-            q, ct = divmod(unit, 8)
-            if unit == 0:
-                both = sb.tile([P, 2, 4, 512], F32, name="st0", tag="x0", align_bytes=64)
-                tiles["st", 0], tiles["st", 1] = both[:, 0], both[:, 1]
-            if unit in (8, 12):
-                tiles["st", unit // 4] = sb.tile([P, 4, 512], F32, name="st2", tag="g%d" % (unit // 4 - 2))[:]
-            st = tiles["st", (unit // 4) % 4]
-            c0 = min(512 * q, DD - 512)
-            n = c0 + 512 - 512 * q
-            tag = tags[unit % len(tags)]
-            bank = zbank(F32, "dwz") if tag == "z" else ps.tile([P, 512], F32, name="dwb", tag=tag)
-            for g in range(2):
-                sl = slice(1024 * g + 128 * ct, 1024 * g + 128 * (ct + 1))
-                PE.matmul_mx(out=bank[:], lhsT=gsc[:, sl].bitcast(E5), lhsT_scale=gss[:, sl], rhs=xc[g][:, c0:c0 + 512].bitcast(E4),
-                             rhs_scale=xs[g][:, c0:c0 + 512], start=(g == 0), stop=(g == 1))
-            S.copy(out=st[:, ct % 4, 0:n], in_=bank[:, 512 - n:512])
-            if ct % 2 == 1:
-                nc.sync.dma_start(out=out_1[128 * (ct - 1):128 * (ct + 1), 512 * q:512 * q + n].rearrange("(c p) w -> p c w", c=2),
-                                  in_=st[:, ct % 4 - 1:ct % 4 + 1, 0:n])
-
-        Q2G = {(1, c) for c in range(0, 5)}
-        chunks = [(g, c) for g in range(2) for c in range(5)]
-        wf = [lambda m=m: w_fill(m // 5, m % 5) for m in range(10)]
-        fills = {0: [lambda: gt_fill(0), lambda: gt_fill(1)], 1: wf[0:4], 2: wf[4:8], 3: wf[8:10],
-                 5: [lambda: gs_fill(0), lambda: gs_fill(1), lambda: gs_fill(2), lambda: gs_fill(3)],
-                 6: [lambda: gt_fill(2), lambda: gt_fill(3)]}
-        pending = []
-        rows = {}
-        fwd_a(0, 0)
-        make_sjn(0)
-        late_consts()
-        fwd_r(0, 0)
-        for s in range(11):
-            if s + 1 < 10:
-                fwd_a(*chunks[s + 1])
-                if s == 3:
-                    make_sjn(1)
-                fwd_r(*chunks[s + 1])
-            if s >= 1:
-                fwd_x(*chunks[s - 1])
-            for q in pending:
-                q()
-            if s == 4:
-                make_t()
-                dx(0)
-            if s == 6:
-                for q in range(5):
-                    x_quant(0, q)
-            if s == 7:
-                x_quant(1, 0)
-            if s == 9:
-                x_quant(1, 1)
-            pending = [fl_() for fl_ in fills.get(s, [])]
-            if s < 10:
-                fwd_q(*chunks[s])
-            if 4 <= s <= 4 + 4:
-                tau = s - 4 - 1
-                if tau >= 0:
-                    m_pass(tau)
-                    if s >= 7:
-                        for u in range(4):
-                            dw(4 * (s - 7) + u, ("dw", "z"))
-                    dx(tau + 1)
-                    u_pass(tau)
-                    rows[tau] = ROWS
-                    if tau > 0:
-                        t_sum(tau - 1, 0, ROWS, ROWS)
-                    if tau == 4:
-                        back(0, 4)
-        t0 = 4
-        unit = 4 * (t0 - 2)
-        m_pass(t0)
-        for q in range(2, 5):
-            x_quant(1, q)
-        for tau in range(t0, 8):
-            if tau > t0:
-                m_pass(tau)
-            if tau in ():
-                u_pass(tau, G)
-                rows[tau] = ROWS
-            n = rows[tau - 1]
-            for step in range(3):
-                if tau < 7:
-                    dx(tau + 1, (step,))
-                dw(unit, ("dw", "cst"))
-                dw(unit + 1, ("dw", "cst"))
-                unit = unit + 2
-                if step == 2:
-                    t_sum(tau - 1, 0, n, n)
-            if tau == 4:
-                back(0, 4)
-            if tau == 7:
-                back(4, 7)
-            if tau not in ():
-                u_pass(tau)
-                rows[tau] = fold(tau, V if tau == 7 else G, fold(tau, V if tau == 7 else G, ROWS))
-            if tau == 5:
+        def sample_tile(tile, units):
+            if tile > 0:
+                fold_terms(tile - 1)
+            make_terms(tile)
+            for bk in range(len(BANKS)):
+                if tile + 1 < PARKED[0]:
+                    dx_bank(tile + 1, bk)
+                dw_units(len(range(bk, units, len(BANKS))))
+                if bk == 1 and tile > 0:
+                    sum_terms(tile - 1)
+                    if tile == 4:
+                        turn_back(0, 4)
+                    if tile == TILES - 1:
+                        turn_back(4, TILES - 1)
+            if tile == 5:
                 finish(0, 4)
-        finish(4, 7)
-        for unit in range(unit, 36):
-            dw(unit, ("dw", "cst", "z"))
-        t_sum(7, 0, rows[7], rows[7])
-        back(7, 8)
-        for unit in range(36, 40):
-            dw(unit, ("dw", "cst", "z"))
-        finish(7, 8)
+
+        steps = [(g, step) for g in range(2) for step in range(len(STEPS))]
+        by_class = [lambda n=n: fill_g_by_class(n) for n in range(4)]
+        by_sample = [lambda n=n: fill_g_by_sample(n) for n in range(4)]
+        fills = (by_class[0:2] + by_sample[0:2]
+                 + [lambda n=n: fill_w(n // W_PIECES, n % W_PIECES) for n in range(2 * W_PIECES)]
+                 + by_sample[2:4] + by_class[2:4])
+        pending = []
+        forward_root(0, 0)
+        make_sgn_col(0)
+        make_backward_vectors()
+        tile = 0
+        for n, (g, step) in enumerate(steps):
+            if n + 1 < len(steps):
+                forward_root(*steps[n + 1])
+            forward_sign(g, step, lambda band: by_col(sgn_col[:, g], band))
+            for call in pending:
+                call()
+            if n == len(STEPS) - 2:
+                make_sgn_col(1)
+            forward_sign(g, step, lambda band: by_row(sgn_row[:, g], band))
+            if n == len(STEPS) - 1:
+                tiles["terms"] = sb.tile([P, 2, TERM_COLS], F32, name="terms", tag="w1", align_bytes=64)
+                V.memset(tiles["terms"][:, :, ROWS * 2 * D:TERM_COLS], 0.0)
+                count["rotating"] = len(rotation) - len(BANKS)
+                for bk in range(len(BANKS)):
+                    dx_bank(0, bk)
+            if n == len(STEPS):
+                for xt in range(X_TILES):
+                    quantise_x(0, xt)
+            if g == 1 and step >= 2:
+                quantise_x(1, step - 2)
+            pending = [fill() for fill in fills[STAGES * n:STAGES * (n + 1)]]
+            forward_x(g, step)
+            if g == 1 and step < len(PARKED):
+                park_dx(PARKED[step])
+            if n in EARLY_TILES:
+                sample_tile(tile, EARLY_TILES[n])
+                tile = tile + 1
+        for xt in range(len(STEPS) - 2, X_TILES):
+            quantise_x(1, xt)
+        for tile in range(4, TILES):
+            sample_tile(tile, LATE_UNITS)
+        finish(4, TILES - 1)
+        fold_terms(TILES - 1)
+        dw_units(X_TILES * C // P - LAST_UNITS - count["unit"])
+        sum_terms(TILES - 1)
+        turn_back(TILES - 1, TILES)
+        dw_units(LAST_UNITS)
+        finish(TILES - 1, TILES)

@@ -78,8 +78,6 @@ def tile_bcnnresnet_v_kernel(tc, feat, W, b, norm, grad_out, out_0, out_1):
         for dst, src, h in ((g_raw, grad_out, 0), (w_raw, W, 0), (w_raw, W, 1), (g_raw, grad_out, 1)):
             nc.sync.dma_start(out=dst[h][:], in_=src[N * h:N * (h + 1), :].rearrange("(p t) c -> p t c", t=4))
 
-        ident_bf = sb.tile([P, P], BF16, name="ident_bf")
-        make_identity(nc, ident_bf[:])
         ident_f32 = sb.tile([P, P], F32, name="ident_f32")
         make_identity(nc, ident_f32[:])
 
@@ -176,50 +174,27 @@ def tile_bcnnresnet_v_kernel(tc, feat, W, b, norm, grad_out, out_0, out_1):
         def fill_g_by_sample(piece):
             g, half = divmod(piece, 2)
             stage = next_stage()
-            if g == 0:
-                S.copy(out=stage[:].rearrange("p (c i t) -> p c t i", i=4, t=4),
-                       in_=g_raw[g][:, :, N * half:N * (half + 1)].rearrange("p t (c i) -> p c t i", i=4))
-            else:
-                for h in range(2):
-                    bank = psum_bank(BF16, "gs_bank")
-                    for m in range(2):
-                        c0 = N * half + 2 * P * h + P * m
-                        PE.matmul(out=bank[:, N * m:N * (m + 1)].rearrange("p (c t) -> p c t", t=4), lhsT=ident_bf[:],
-                                  rhs=g_raw[g][:, :, c0:c0 + P].rearrange("p t c -> p c t"), start=True, stop=True)
-                    S.copy(out=stage[:, 2 * N * h:2 * N * (h + 1)].bitcast(F32), in_=bank[:].bitcast(F32))
+            S.copy(out=stage[:].rearrange("p (c i t) -> p c t i", i=4, t=4),
+                   in_=g_raw[g][:, :, N * half:N * (half + 1)].rearrange("p t (c i) -> p c t i", i=4))
             cols = slice(N * piece, N * (piece + 1))
             return lambda: quantise(stage[:], gs_codes[:, cols], gs_scales[:, cols], E5)
 
         def fill_w(kp, piece):
             stage = next_stage()
-            by_pair = w_raw[kp][:].rearrange("p t (r e j) -> p r e j t", e=2, j=D)
-            mirrored = w_raw[kp][:].rearrange("p t (j i) -> p j i t", i=D)
+            copy = V.tensor_copy if piece < len(BANKS) and kp == 1 else S.copy
             halves = stage[:, 0:8 * KB].rearrange("p (e k t) -> p e k t", e=2, t=4)
-            bk, half = piece % len(BANKS), KB // 2
-            for h in range(2):
-                bank = psum_bank(BF16, "w_bank")
+            bk = piece % len(BANKS)
+            for band in BANKS[bk]:
+                k0, w, i0 = band_start(band) - KB * bk, width(band), BAND * band
+                dst = halves[:, :, k0:k0 + PAIRS * w, :]
                 if piece < len(BANKS):
-                    view = bank[:, 0:4 * KB].rearrange("p (k t) -> p k t", t=4)
-                    for band in BANKS[bk]:
-                        k0, w = band_start(band) - KB * bk, width(band)
-                        for r in range(0, PAIRS, 2):
-                            PE.matmul(out=view[:, k0 + r * w:k0 + (r + 2) * w, :].rearrange("p (r j) t -> p r j t", r=2),
-                                      lhsT=ident_bf[:], rhs=by_pair[:, PAIRS * band + r:PAIRS * band + r + 2, h, D - w:D, :],
-                                      start=True, stop=True)
-                    S.copy(out=halves[:, h].bitcast(F32), in_=view.bitcast(F32))
+                    src = w_raw[kp][:].rearrange("p t (r e j) -> p e r t j", e=2, j=D)[:, :, PAIRS * band:PAIRS * (band + 1), :, i0:D]
+                    for e in range(2):
+                        copy(out=dst[:, e].rearrange("p (r c i) t -> p r c t i", r=PAIRS, i=4),
+                             in_=src[:, e].rearrange("p r t (c i) -> p r c t i", i=4))
                 else:
-                    view = bank[:, 0:4 * KB].rearrange("p (k e t) -> p k e t", e=2, t=4)
-                    for band in BANKS[bk]:
-                        w = width(band)
-                        for r in range(PAIRS):
-                            k0 = band_start(band) - KB * bk + r * w - half * h
-                            lo, hi = max(k0, 0), min(k0 + w, half)
-                            i0 = BAND * band + 2 * r
-                            if lo < hi:
-                                PE.matmul(out=view[:, lo:hi], lhsT=ident_bf[:],
-                                          rhs=mirrored[:, D - w + lo - k0:D - w + hi - k0, i0:i0 + 2, :], start=True, stop=True)
-                    S.copy(out=halves[:, :, half * h:half * (h + 1), :].bitcast(F32),
-                           in_=view.bitcast(F32).rearrange("p k e t -> p e k t"))
+                    src = w_raw[kp][:].rearrange("p t (j i) -> p j t i", i=D)[:, i0:D, :, i0:i0 + BAND]
+                    copy(out=dst.rearrange("p e (r j) t -> p r j t e", r=PAIRS), in_=src.rearrange("p j t (r e) -> p r j t e", e=2))
             cols = slice(2 * KB * piece, 2 * KB * piece + N)
             return lambda: quantise(stage[:], w_codes[kp][:, cols], w_scales[kp][:, cols], E4)
 

from contextlib import ExitStack

import concourse.mybir as mybir
from concourse.masks import make_identity

B, D, C = 1024, 48, 1024
DD = D * D
FLOPS = 2 * 2 * B * C * DD
BYTES = 2 * B * D + 2 * C * DD + 4 * B + 2 * B * C + 4 * B * D + 4 * C * DD
EPS = 1e-10
TINY = 2.0 ** -32

F32 = mybir.dt.float32
BF16 = mybir.dt.bfloat16
U32 = mybir.dt.uint32
U8 = mybir.dt.uint8
E4 = mybir.dt.float8_e4m3fn_x4
E5 = mybir.dt.float8_e5m2_x4
ALU = mybir.AluOpType
ACT = mybir.ActivationFunctionType
AX = mybir.AxisListType

P = 128
N = 512
TILES = 8
BAND = 8
BANDS = D // BAND
PAIRS = BAND // 2
BANKS = [[0, 5], [1, 4], [2, 3]]
KB = PAIRS * (2 * D - BAND * (BANDS - 1))
KALL = len(BANKS) * KB
STEPS = [[0], [1], [2], [3], [4, 5]]
W_PIECES = 2 * len(BANKS)
W_COLS = W_PIECES * 2 * KB + N - 2 * KB
ROWS = D // 2
TERM_COLS = ROWS * 2 * D + P - 2 * D
X_TILES = 5
STAGES = 4
PARKED = [6, 7]
SCALAR_BANDS = [4, 2]
EARLY_TILES = {4: 0, 5: 0, 7: 8, 8: 8}
LATE_UNITS = 5
LAST_UNITS = 3


def width(band):
    return D - BAND * band


def band_start(band):
    order = [o for bank in BANKS for o in bank]
    return sum(PAIRS * width(o) for o in order[:order.index(band)])


def tile_bcnnresnet_v_kernel(tc, feat, W, b, norm, grad_out, out_0, out_1):
    nc = tc.nc
    V, S, PE = nc.vector, nc.scalar, nc.tensor
    with ExitStack() as ctx:
        sb = ctx.enter_context(tc.tile_pool(name="sb", bufs=1))
        ps = ctx.enter_context(tc.psum_pool(name="ps", bufs=1))
        tiles = {}
        count = {"bank": 0, "stage": 0, "unit": 0, "rotating": 7}

        rotation = ["f0", "f1", "f2", "f3", "z0", "z1", "z2"]

        def psum_bank(dtype, name, tag=None):
            if tag is None:
                count["bank"] = count["bank"] + 1
                tag = rotation[count["bank"] % count["rotating"]]
            return ps.tile([P, N if dtype == F32 else 2 * N], dtype, name=name, tag=tag)

        f = sb.tile([P, 2, 4, D], BF16, name="f", tag="f")
        nc.sync.dma_start(out=f[:], in_=feat.rearrange("(g p t) d -> p g t d", g=2, t=4))
        nrm = sb.tile([P, 2, 4], F32, name="nrm")
        nc.sync.dma_start(out=nrm[:], in_=norm.rearrange("(g p t) -> p g t", g=2, t=4))
        g_raw = [sb.tile([P, 4, C], BF16, name="g_raw%d" % g, tag="g%d" % g) for g in range(2)]
        w_raw = [sb.tile([P, 4, DD], BF16, name="w_raw%d" % kp, tag="w%d" % kp, align_bytes=64) for kp in range(2)]
        for dst, src, h in ((g_raw, grad_out, 0), (w_raw, W, 0), (w_raw, W, 1), (g_raw, grad_out, 1)):
            nc.sync.dma_start(out=dst[h][:], in_=src[N * h:N * (h + 1), :].rearrange("(p t) c -> p t c", t=4))

        ident_f32 = sb.tile([P, P], F32, name="ident_f32")
        make_identity(nc, ident_f32[:])

        f_flat = f[:].rearrange("p g t d -> p (g t d)")
        mag = sb.tile([P, TILES * D], BF16, name="mag")
        S.activation(out=mag[:], in_=f_flat, func=ACT.Abs)
        mag_row = sb.tile([P, 2, ROWS, 4, 2], BF16, name="mag_row")
        S.copy(out=mag_row[:], in_=mag[:].rearrange("p (g t r e) -> p g r t e", g=2, t=4, e=2))
        mag_col = sb.tile([P, 2, D, 4, 2], BF16, name="mag_col")
        S.copy(out=mag_col[:],
               in_=mag[:].rearrange("p (g t j) -> p g j t", g=2, t=4).unsqueeze(4).to_broadcast([P, 2, D, 4, 2]))
        sgn = sb.tile([P, TILES * D], BF16, name="sgn")
        S.activation(out=sgn[:], in_=f_flat, func=ACT.Sign)
        tiny_at_0 = sb.tile([P, TILES * D], BF16, name="tiny_at_0", tag="small0")
        V.tensor_scalar(out=tiny_at_0[:], in0=f_flat, scalar1=0.0, scalar2=TINY, op0=ALU.is_equal, op1=ALU.mult)
        inv_norm = sb.tile([P, TILES], F32, name="inv_norm")
        V.reciprocal(out=inv_norm[:], in_=nrm[:].rearrange("p g t -> p (g t)"))
        top = sb.tile([P, 2], F32, name="top")
        V.tensor_reduce(out=top[:], in_=mag[:].rearrange("p (g m) -> p g m", g=2), axis=AX.X, op=ALU.max)
        sgn_tiny = sb.tile([P, TILES * D], BF16, name="sgn_tiny", tag="small1")
        V.tensor_tensor(out=sgn_tiny[:], in0=sgn[:], in1=tiny_at_0[:], op=ALU.add)
        V.tensor_scalar(out=top[:], in0=top[:], scalar1=EPS ** 0.5, scalar2=0.25, op0=ALU.max, op1=ALU.mult)
        nu = sb.tile([P, 2], F32, name="nu")
        V.reciprocal(out=nu[:], in_=top[:])
        nu2 = sb.tile([P, 2], F32, name="nu2")
        V.tensor_tensor(out=nu2[:], in0=nu[:], in1=nu[:], op=ALU.mult)
        nu_norm = sb.tile([P, 2, 4], F32, name="nu_norm")
        V.tensor_tensor(out=nu_norm[:], in0=inv_norm[:].rearrange("p (g t) -> p g t", g=2),
                        in1=nu[:].unsqueeze(2).to_broadcast([P, 2, 4]), op=ALU.mult)
        eps_nu2 = sb.tile([P, 2], F32, name="eps_nu2")
        V.tensor_scalar(out=eps_nu2[:], in0=nu2[:], scalar1=EPS, scalar2=None, op0=ALU.mult)
        sgn_row = sb.tile([P, 2, ROWS, 4, 2], BF16, name="sgn_row")
        S.copy(out=sgn_row[:], in_=sgn_tiny[:].rearrange("p (g t r e) -> p g r t e", g=2, t=4, e=2))
        sgn_col = sb.tile([P, 2, D, 4, 2], F32, name="sgn_col")

        def make_sgn_col(g):
            V.tensor_tensor(out=sgn_col[:, g],
                            in0=sgn_tiny[:].rearrange("p (g t j) -> p g j t", g=2, t=4)[:, g].unsqueeze(3)
                            .to_broadcast([P, D, 4, 2]),
                            in1=nu_norm[:, g].unsqueeze(1).unsqueeze(3).to_broadcast([P, D, 4, 2]), op=ALU.mult)

        mag32 = sb.tile([P, TILES, D], F32, name="mag32")
        half_inv_sgn = sb.tile([P, TILES * D], BF16, name="half_inv_sgn")
        sgn_sum = sb.tile([P, TILES, D], F32, name="sgn_sum")

        def make_backward_vectors():
            mag_sum = sb.tile([P, TILES], F32, name="mag_sum")
            for n in range(TILES):
                S.activation(out=mag32[:, n, :], in_=mag[:, D * n:D * (n + 1)], func=ACT.Copy, accum_out=mag_sum[:, n:n + 1])
            big_at_0 = sb.tile([P, TILES * D], BF16, name="big_at_0", tag="small2")
            V.tensor_scalar(out=big_at_0[:], in0=f_flat, scalar1=0.0, scalar2=0.5 / TINY, op0=ALU.is_equal, op1=ALU.mult)
            k1 = sb.tile([P, TILES], F32, name="k1")
            V.scalar_tensor_tensor(out=k1[:], in0=mag_sum[:], scalar=0.5, in1=inv_norm[:], op0=ALU.mult, op1=ALU.mult)
            V.scalar_tensor_tensor(out=half_inv_sgn[:], in0=sgn[:], scalar=0.5, in1=big_at_0[:], op0=ALU.mult, op1=ALU.add)
            k2 = sb.tile([P, TILES], F32, name="k2")
            V.tensor_tensor(out=k2[:], in0=k1[:], in1=inv_norm[:], op=ALU.mult)
            for n in range(TILES):
                S.activation(out=sgn_sum[:, n, :], in_=sgn[:, D * n:D * (n + 1)], func=ACT.Copy, scale=k2[:, n:n + 1])

        q_all = [sb.tile([P, KALL, 4, 2], F32, name="q%d" % g) for g in range(2)]
        stages = [sb.tile([P, 4 * N], BF16, name="stage%d" % i, align_bytes=64) for i in range(STAGES)]
        w_codes = [sb.tile([P, W_COLS], U32, name="w_codes%d" % i, align_bytes=64) for i in range(2)]
        w_scales = [sb.tile([P, W_COLS], U8, name="w_scales%d" % i, align_bytes=64) for i in range(2)]
        gc_codes = sb.tile([P, 4 * N], U32, name="gc_codes", align_bytes=64)
        gc_scales = sb.tile([P, 4 * N], U8, name="gc_scales", align_bytes=64)
        gs_codes = sb.tile([P, 4 * N], U32, name="gs_codes", align_bytes=64)
        gs_scales = sb.tile([P, 4 * N], U8, name="gs_scales", align_bytes=64)
        x_codes = [sb.tile([P, DD], U32, name="x_codes%d" % i, align_bytes=64) for i in range(2)]
        x_scales = [sb.tile([P, DD], U8, name="x_scales%d" % i, align_bytes=64) for i in range(2)]
        m_sums = sb.tile([P, TILES, len(BANKS) + BANDS], F32, name="m_sums")

        def next_stage():
            count["stage"] = count["stage"] + 1
            return stages[(count["stage"] - 1) % STAGES]

        def quantise(src, codes, scales, fmt):
            V.quantize_mx(out=codes.bitcast(fmt), scales=scales, in_=src)

        def fill_g_by_class(pair):
            stage = next_stage()
            for h in range(2):
                tile = 2 * pair + h
                words = g_raw[tile // 4][:, tile % 4, :].bitcast(F32)
                bank = psum_bank(F32, "gc_bank")
                for kp in range(2):
                    for u in range(2):
                        PE.transpose(bank[:, P * (2 * kp + u):P * (2 * kp + u + 1)],
                                     words[:, 2 * P * kp + u:2 * P * (kp + 1):2], ident_f32[:])
                S.copy(out=stage[:, 2 * N * h:2 * N * (h + 1)].bitcast(F32).rearrange("p (k n u) -> p k n u", k=2, u=2),
                       in_=bank[:].rearrange("p (k u n) -> p k n u", k=2, u=2))
            cols = slice(N * pair, N * (pair + 1))
            return lambda: quantise(stage[:], gc_codes[:, cols], gc_scales[:, cols], E5)

        def fill_g_by_sample(piece):
            g, half = divmod(piece, 2)
            stage = next_stage()
            S.copy(out=stage[:].rearrange("p (c i t) -> p c t i", i=4, t=4),
                   in_=g_raw[g][:, :, N * half:N * (half + 1)].rearrange("p t (c i) -> p c t i", i=4))
            cols = slice(N * piece, N * (piece + 1))
            return lambda: quantise(stage[:], gs_codes[:, cols], gs_scales[:, cols], E5)

        def fill_w(kp, piece):
            stage = next_stage()
            copy = V.tensor_copy if piece < len(BANKS) and kp == 1 else S.copy
            halves = stage[:, 0:8 * KB].rearrange("p (e k t) -> p e k t", e=2, t=4)
            bk = piece % len(BANKS)
            for band in BANKS[bk]:
                k0, w, i0 = band_start(band) - KB * bk, width(band), BAND * band
                dst = halves[:, :, k0:k0 + PAIRS * w, :]
                if piece < len(BANKS):
                    src = w_raw[kp][:].rearrange("p t (r e j) -> p e r t j", e=2, j=D)[:, :, PAIRS * band:PAIRS * (band + 1), :, i0:D]
                    for e in range(2):
                        copy(out=dst[:, e].rearrange("p (r c i) t -> p r c t i", r=PAIRS, i=4),
                             in_=src[:, e].rearrange("p r t (c i) -> p r c t i", i=4))
                else:
                    src = w_raw[kp][:].rearrange("p t (j i) -> p j t i", i=D)[:, i0:D, :, i0:i0 + BAND]
                    copy(out=dst.rearrange("p e (r j) t -> p r j t e", r=PAIRS), in_=src.rearrange("p j t (r e) -> p r j t e", e=2))
            cols = slice(2 * KB * piece, 2 * KB * piece + N)
            return lambda: quantise(stage[:], w_codes[kp][:, cols], w_scales[kp][:, cols], E4)

        def shaped(ap, band, k0):
            return ap[:, k0:k0 + PAIRS * width(band)].rearrange("p (r j) t e -> p r j t e", r=PAIRS)

        def step_bands(step):
            return [(band, sum(PAIRS * width(o) for o in STEPS[step][:n])) for n, band in enumerate(STEPS[step])]

        def by_row(vec, band):
            return vec[:, PAIRS * band:PAIRS * (band + 1)].unsqueeze(2).to_broadcast([P, PAIRS, width(band), 4, 2])

        def by_col(vec, band):
            return vec[:, D - width(band):D].unsqueeze(1).to_broadcast([P, PAIRS, width(band), 4, 2])

        def forward_root(g, step):
            prod = sb.tile([P, PAIRS * D, 4, 2], F32, name="prod", tag="prod", bufs=2)
            tiles["prod", g, step] = prod
            for band, k0 in step_bands(step):
                V.tensor_tensor(out=shaped(prod, band, k0), in0=by_col(mag_col[:, g], band), in1=by_row(mag_row[:, g], band),
                                op=ALU.mult)
            for band, k0 in step_bands(step):
                S.activation(out=shaped(q_all[g], band, band_start(band)), in_=shaped(prod, band, k0),
                             func=ACT.Abs_reciprocal_sqrt, bias=eps_nu2[:, g:g + 1], scale=nu2[:, g:g + 1])

        def forward_sign(g, step, factor):
            for band in STEPS[step]:
                q = shaped(q_all[g], band, band_start(band))
                V.tensor_tensor(out=q, in0=q, in1=factor(band), op=ALU.mult)

        def forward_x(g, step):
            if step == 0:
                tiles["x", g] = sb.tile([P, DD, 4], BF16, name="x%d" % g, tag=("x0", "w0")[g], align_bytes=64)
            by_pair = tiles["x", g][:].rearrange("p (r e j) t -> p r e j t", e=2, j=D)
            square = tiles["x", g][:].rearrange("p (i j) t -> p i j t", j=D)
            for band, k0 in step_bands(step):
                prod, q = shaped(tiles["prod", g, step], band, k0), shaped(q_all[g], band, band_start(band))
                i0, i1 = BAND * band, BAND * (band + 1)
                for e in range(2):
                    V.scalar_tensor_tensor(out=by_pair[:, PAIRS * band:PAIRS * (band + 1), e, i0:D, :], in0=prod[:, :, :, :, e],
                                           scalar=EPS, in1=q[:, :, :, :, e], op0=ALU.add, op1=ALU.mult)
                if i1 < D:
                    S.copy(out=square[:, i1:D, i0:i1, :], in_=square[:, i0:i1, i1:D, :].rearrange("p i j t -> p j i t"))

        def quantise_x(g, xt):
            cols = slice(N * xt, min(N * (xt + 1), DD))
            quantise(tiles["x", g][:, cols, :].rearrange("p c t -> p (c t)"), x_codes[g][:, cols], x_scales[g][:, cols], E4)

        def dx_bank(tile, bk):
            bank = psum_bank(F32, "dx_bank", None if tile in PARKED else "z%d" % bk)
            passes = [(kp, piece) for piece in (bk, bk + len(BANKS)) for kp in range(2)]
            for n, (kp, piece) in enumerate(passes):
                samples = slice(2 * P * tile + P * kp, 2 * P * tile + P * (kp + 1))
                cols = slice(2 * KB * piece, 2 * KB * piece + N)
                PE.matmul_mx(out=bank[:], lhsT=gc_codes[:, samples].bitcast(E5), lhsT_scale=gc_scales[:, samples],
                             rhs=w_codes[kp][:, cols].bitcast(E4), rhs_scale=w_scales[kp][:, cols],
                             start=(n == 0), stop=(n == len(passes) - 1))
            tiles["dx", tile, bk] = bank[:, 0:2 * KB].rearrange("p (e k) -> p k e", e=2)

        def park_dx(tile):
            parked = sb.tile([P, KALL, 2], F32, name="parked", tag="g%d" % PARKED.index(tile))
            for bk in range(len(BANKS)):
                dx_bank(tile, bk)
                S.copy(out=parked[:, KB * bk:KB * (bk + 1), :], in_=tiles["dx", tile, bk])
                tiles["dx", tile, bk] = parked[:, KB * bk:KB * (bk + 1), :]

        def make_terms(tile):
            g, t = divmod(tile, 4)
            m = sb.tile([P, KALL, 2], F32, name="m", tag="m", bufs=2)
            for bk in range(len(BANKS)):
                ks = slice(KB * bk, KB * (bk + 1))
                V.scalar_tensor_tensor(out=m[:, ks, :], in0=tiles["dx", tile, bk], scalar=1.0, in1=q_all[g][:, ks, t, :],
                                       op0=ALU.mult, op1=ALU.mult, accum_out=m_sums[:, tile, bk:bk + 1])
            rows = tiles["terms"][:, tile % 2, 0:ROWS * 2 * D].rearrange("p (r s m) -> p r s m", s=2, m=D)
            a = mag32[:, tile]
            for band in [o for bank in BANKS for o in bank]:
                w, k0, r0, i0 = width(band), band_start(band), PAIRS * band, BAND * band
                mb = m[:, k0:k0 + PAIRS * w, :].rearrange("p (r j) e -> p r j e", r=PAIRS)
                if band < SCALAR_BANDS[g]:
                    for i in range(BAND):
                        S.activation(out=rows[:, r0 + i // 2, i % 2, i0:D], in_=mb[:, i // 2, :, i % 2], func=ACT.Copy,
                                     scale=a[:, i0 + i:i0 + i + 1])
                else:
                    V.tensor_tensor(out=rows[:, r0:r0 + PAIRS, :, i0:D], in0=mb.rearrange("p r j e -> p r e j"),
                                    in1=a[:, i0:i0 + BAND].rearrange("p (r e) -> p r e", e=2).unsqueeze(3)
                                    .to_broadcast([P, PAIRS, 2, w]), op=ALU.mult)
                if w > BAND:
                    below = rows[:, r0 + PAIRS:ROWS].rearrange("p r s m -> p (r s) m")[:, :, i0:i0 + BAND]
                    V.tensor_tensor(out=below.rearrange("p j (r e) -> p j r e", e=2),
                                    in0=mb[:, :, BAND:w, :].rearrange("p r j e -> p j r e"),
                                    in1=a[:, i0 + BAND:D].unsqueeze(2).unsqueeze(3).to_broadcast([P, w - BAND, PAIRS, 2]),
                                    op=ALU.mult)
                unread = sb.tile([P, PAIRS, BAND, 2], F32, name="unread", tag="unread")
                S.activation(out=unread[:], in_=mb[:, :, 0:BAND, :], func=ACT.Copy, scale=-0.5,
                             accum_out=m_sums[:, tile, len(BANKS) + band:len(BANKS) + band + 1])

        def fold_terms(tile):
            terms = tiles["terms"][:, tile % 2, :]
            rows = ROWS
            for n in range(tile // 4 + tile // (TILES - 1)):
                rows = rows // 2
                V.tensor_tensor(out=terms[:, 0:2 * D * rows], in0=terms[:, 0:2 * D * rows],
                                in1=terms[:, 2 * D * rows:4 * D * rows], op=ALU.add)
            tiles["rows", tile] = rows

        def sum_terms(tile):
            g, t = divmod(tile, 4)
            if t == 0:
                tiles["acc", g] = psum_bank(F32, "acc", "acc")
            terms, rows = tiles["terms"][:, tile % 2, :], tiles["rows", tile]
            for r in range(rows):
                PE.matmul(out=tiles["acc", g][:, P * t:P * (t + 1)], lhsT=terms[:, 2 * D * r:2 * D * r + P], rhs=ident_f32[:],
                          start=(r == 0), stop=(r == rows - 1), is_transpose=True)

        def turn_back(t0, t1):
            n = t1 - t0
            sums = sb.tile([P, n, P], F32, name="sums", tag="sums")
            S.copy(out=sums[:], in_=tiles["acc", t0 // 4][:, P * (t0 % 4):P * (t0 % 4 + n)].rearrange("p (t n) -> p t n", n=P))
            bank = psum_bank(F32, "back")
            for t in range(n):
                PE.transpose(bank[:, 2 * D * t:2 * D * t + P], sums[:, t, :], ident_f32[:])
            tiles["back", t0] = bank

        def finish(t0, t1):
            g, n = t0 // 4, t1 - t0
            cols = slice(D * t0, D * t1)
            b_sum = sb.tile([P, n * D], F32, name="b_sum", tag="small2")
            V.tensor_reduce(out=b_sum[:].rearrange("p (t m) -> p t m", m=D),
                            in_=tiles["back", t0][:, 0:2 * D * n].rearrange("p (t s m) -> p t m s", s=2, m=D),
                            axis=AX.X, op=ALU.add)
            m_half = sb.tile([P, n], F32, name="m_half", tag="m_half")
            V.tensor_reduce(out=m_half[:], in_=m_sums[:, t0:t1, :], axis=AX.X, op=ALU.add)
            ab = sb.tile([P, n, D], F32, name="ab", tag="small0")
            V.tensor_tensor(out=ab[:].rearrange("p t m -> p (t m)"), in0=b_sum[:], in1=mag[:, cols], op=ALU.mult)
            first = sb.tile([P, n * D], F32, name="first", tag="f")
            V.tensor_tensor(out=first[:], in0=b_sum[:], in1=half_inv_sgn[:, cols], op=ALU.mult)
            ab_sum = sb.tile([P, n], F32, name="ab_sum", tag="ab_sum")
            V.tensor_reduce(out=ab_sum[:], in_=ab[:], axis=AX.X, op=ALU.add)
            dot2 = sb.tile([P, n], F32, name="dot2", tag="dot2")
            V.scalar_tensor_tensor(out=dot2[:], in0=m_half[:], scalar=2 * EPS, in1=ab_sum[:], op0=ALU.mult, op1=ALU.add)
            V.tensor_tensor(out=ab[:], in0=sgn_sum[:, t0:t1, :], in1=dot2[:].unsqueeze(2).to_broadcast([P, n, D]), op=ALU.mult)
            res = sb.tile([P, n, D], F32, name="res", tag="small1" if t1 < TILES else "res")
            V.tensor_tensor(out=res[:].rearrange("p t m -> p (t m)"), in0=first[:], in1=ab[:].rearrange("p t m -> p (t m)"),
                            op=ALU.subtract)
            nc.sync.dma_start(out=out_0[N * g:N * (g + 1), :].rearrange("(p t) d -> p t d", t=4)[:, t0 % 4:t0 % 4 + n, :],
                              in_=res[:])

        def dw_units(n):
            for unit in range(count["unit"], count["unit"] + n):
                xt, ct = divmod(unit, C // P)
                if unit == 0:
                    tiles["out"] = sb.tile([P, C // P, N], F32, name="out", tag="x0", align_bytes=64)
                c0 = min(N * xt, DD - N)
                new = c0 + N - N * xt
                bank = psum_bank(F32, "dw_bank")
                for g in range(2):
                    classes = slice(C * g + P * ct, C * g + P * (ct + 1))
                    PE.matmul_mx(out=bank[:], lhsT=gs_codes[:, classes].bitcast(E5), lhsT_scale=gs_scales[:, classes],
                                 rhs=x_codes[g][:, c0:c0 + N].bitcast(E4), rhs_scale=x_scales[g][:, c0:c0 + N],
                                 start=(g == 0), stop=(g == 1))
                S.copy(out=tiles["out"][:, ct, 0:new], in_=bank[:, N - new:N])
                if ct % 2 == 1:
                    nc.sync.dma_start(out=out_1[P * (ct - 1):P * (ct + 1), N * xt:N * xt + new].rearrange("(c p) w -> p c w", c=2),
                                      in_=tiles["out"][:, ct - 1:ct + 1, 0:new])
            count["unit"] = count["unit"] + n

        def sample_tile(tile, units):
            if tile > 0:
                fold_terms(tile - 1)
            make_terms(tile)
            for bk in range(len(BANKS)):
                if tile + 1 < PARKED[0]:
                    dx_bank(tile + 1, bk)
                dw_units(len(range(bk, units, len(BANKS))))
                if bk == 1 and tile > 0:
                    sum_terms(tile - 1)
                    if tile == 4:
                        turn_back(0, 4)
                    if tile == TILES - 1:
                        turn_back(4, TILES - 1)
            if tile == 5:
                finish(0, 4)

        steps = [(g, step) for g in range(2) for step in range(len(STEPS))]
        by_class = [lambda n=n: fill_g_by_class(n) for n in range(4)]
        by_sample = [lambda n=n: fill_g_by_sample(n) for n in range(4)]
        fills = (by_class[0:2] + by_sample[0:2]
                 + [lambda n=n: fill_w(n // W_PIECES, n % W_PIECES) for n in range(2 * W_PIECES)]
                 + by_sample[2:4] + by_class[2:4])
        pending = []
        forward_root(0, 0)
        make_sgn_col(0)
        make_backward_vectors()
        tile = 0
        for n, (g, step) in enumerate(steps):
            if n + 1 < len(steps):
                forward_root(*steps[n + 1])
            forward_sign(g, step, lambda band: by_col(sgn_col[:, g], band))
            for call in pending:
                call()
            if n == len(STEPS) - 2:
                make_sgn_col(1)
            forward_sign(g, step, lambda band: by_row(sgn_row[:, g], band))
            if n == len(STEPS) - 1:
                tiles["terms"] = sb.tile([P, 2, TERM_COLS], F32, name="terms", tag="w1", align_bytes=64)
                V.memset(tiles["terms"][:, :, ROWS * 2 * D:TERM_COLS], 0.0)
                count["rotating"] = len(rotation) - len(BANKS)
                for bk in range(len(BANKS)):
                    dx_bank(0, bk)
            if n == len(STEPS):
                for xt in range(X_TILES):
                    quantise_x(0, xt)
            if g == 1 and step >= 2:
                quantise_x(1, step - 2)
            pending = [fill() for fill in fills[STAGES * n:STAGES * (n + 1)]]
            forward_x(g, step)
            if g == 1 and step < len(PARKED):
                park_dx(PARKED[step])
            if n in EARLY_TILES:
                sample_tile(tile, EARLY_TILES[n])
                tile = tile + 1
        for xt in range(len(STEPS) - 2, X_TILES):
            quantise_x(1, xt)
        for tile in range(4, TILES):
            sample_tile(tile, LATE_UNITS)
        finish(4, TILES - 1)
        fold_terms(TILES - 1)
        dw_units(X_TILES * C // P - LAST_UNITS - count["unit"])
        sum_terms(TILES - 1)
        turn_back(TILES - 1, TILES)
        dw_units(LAST_UNITS)
        finish(TILES - 1, TILES)
